import numpy as np
import ml_dtypes


def mxq(x, axis, fmt="e4m3"):
    dtype, down = {"e4m3": (ml_dtypes.float8_e4m3fn, 7), "e5m2": (ml_dtypes.float8_e5m2, 14)}[fmt]
    v = np.moveaxis(np.asarray(x, np.float32).astype(ml_dtypes.bfloat16).astype(np.float64), axis, -1)
    blocks = v.reshape(v.shape[:-1] + (-1, 32))
    amax = np.abs(blocks).max(-1, keepdims=True)
    byte = np.maximum(np.where(amax > 0, np.frexp(amax)[1] - 1 + 127, 0) - down, 1)
    scale = np.exp2(byte - 127.0)
    codes = (blocks / scale).astype(np.float32).astype(dtype).astype(np.float64)
    return np.moveaxis((codes * scale).reshape(v.shape), -1, axis)


WIDE = False


def mx_kscale(k):
    if not WIDE:
        return np.ones(k)
    levels = np.array([10, -10, 5, -5, 0])
    a = np.random.permutation(np.resize(levels, k // 512 * 4)).reshape(k // 512, 4)
    idx = np.arange(k)
    return np.exp2(a[idx // 512, idx % 128 // 32])


BF16 = ml_dtypes.bfloat16


def bf(x):
    return np.asarray(x, np.float32).astype(BF16)


def f64(x):
    return np.asarray(x).astype(np.float64)


E2M1 = np.array([0.0, 0.5, 1.0, 1.5, 2.0, 3.0, 4.0, 6.0, -0.0, -0.5, -1.0, -1.5, -2.0, -3.0, -4.0, -6.0])


def pack_weight(w, fmt):
    k, n = w.shape
    w = f64(bf(w)).reshape(k // 32, 32, n)
    amax = np.abs(w).max(1)
    if fmt == "e4m3":
        byte = np.frexp(amax)[1] - 1 + 127 - 7
    else:
        mant, ex = np.frexp(amax / 6.0)
        byte = np.where(mant > 0.5, ex, ex - 1) + 127
    byte = np.clip(np.where(amax > 0, byte, 1), 1, 254)
    scaled = (w * np.exp2(127.0 - byte)[:, None, :]).reshape(k, n).astype(np.float32)
    by_word = np.ascontiguousarray(scaled.reshape(k // 512, 128, 4, n).transpose(0, 1, 3, 2))
    if fmt == "e4m3":
        words = by_word.astype(ml_dtypes.float8_e4m3fn).view(np.uint8)
    else:
        c = by_word.astype(ml_dtypes.float4_e2m1fn).view(np.uint8) & 0xF
        words = c[..., 0::2] | (c[..., 1::2] << 4)
    return np.ascontiguousarray(words), np.ascontiguousarray(byte.astype(np.uint8).reshape(k // 512, 16, n))


def unpack_weight(words, scales, fmt):
    g, p, n, _ = words.shape
    if fmt == "e4m3":
        vals = np.ascontiguousarray(words).view(ml_dtypes.float8_e4m3fn).astype(np.float64)
    else:
        nib = np.empty((g, p, n, 4), np.uint8)
        nib[..., 0::2] = words & 0xF
        nib[..., 1::2] = words >> 4
        vals = E2M1[nib]
    vals = vals * np.repeat(np.exp2(scales.astype(np.float64) - 127.0), 8, axis=1)[..., None]
    return vals.transpose(0, 1, 3, 2).reshape(g * 512, n)


S, E, HQ, HK, D, C = 1024, 1024, 16, 4, 128, 512


def rotate_half(t):
    t1, t2 = np.split(t, 2, axis=-1)
    return np.concatenate([-t2, t1], axis=-1)


def setup_inputs():
    s = mx_kscale(E)
    theta = np.random.uniform(0.0, 2.0 * np.pi, (S, D // 2))
    theta = np.concatenate([theta, theta], axis=-1)
    x = bf(np.random.standard_normal((S, E)) * s)
    w_q = np.random.standard_normal((HQ * D, E)) * 1.4 / np.sqrt(E) / s[None, :]
    w_k = np.random.standard_normal((HK * D, E)) * 1.4 / np.sqrt(E) / s[None, :]
    w_v = np.random.standard_normal((HK * D, E)) / np.sqrt(E) / s[None, :]
    w_q_words, w_q_scales = pack_weight(w_q.T, "e4m3")
    w_k_words, w_k_scales = pack_weight(w_k.T, "e4m3")
    w_v_words, w_v_scales = pack_weight(w_v.T, "e4m3")
    return {"x": x,
            "w_q_words": w_q_words, "w_q_scales": w_q_scales,
            "w_k_words": w_k_words, "w_k_scales": w_k_scales,
            "w_v_words": w_v_words, "w_v_scales": w_v_scales,
            "cos_tab": bf(np.cos(theta)), "sin_tab": bf(np.sin(theta))}


def reference(x, w_q_words, w_q_scales, w_k_words, w_k_scales, w_v_words, w_v_scales, cos_tab, sin_tab):
    xq = mxq(f64(x), 1, "e4m3")
    q = (xq @ unpack_weight(w_q_words, w_q_scales, "e4m3")).reshape(S, HQ, D)
    k = (xq @ unpack_weight(w_k_words, w_k_scales, "e4m3")).reshape(S, HK, D)
    v = (xq @ unpack_weight(w_v_words, w_v_scales, "e4m3")).reshape(S, HK, D)
    c = f64(cos_tab).reshape(S, 1, D)
    sn = f64(sin_tab).reshape(S, 1, D)
    q_rot = q * c + rotate_half(q) * sn
    k_rot = k * c + rotate_half(k) * sn
    return q_rot, k_rot, v

@@ -1,0 +1,167 @@
+from contextlib import ExitStack
+
+import concourse.mybir as mybir
+from concourse.masks import make_identity
+
+F32 = mybir.dt.float32
+BF16 = mybir.dt.bfloat16
+I32 = mybir.dt.int32
+U32 = mybir.dt.uint32
+U8 = mybir.dt.uint8
+FP8X4 = mybir.dt.float8_e4m3fn_x4
+
+P = 128
+ROWS = 1024
+K = 1024
+K_PASS = 4 * P
+PASSES = K // K_PASS
+ROW_SETS = ROWS // P
+HEAD = 128
+HALF = HEAD // 2
+BANK = 512
+HEADS_PER_BANK = BANK // HEAD
+N_Q = 16 * HEAD
+N_KV = 4 * HEAD
+Q_COL, K_COL, V_COL = 0, N_Q, N_Q + N_KV
+N_ALL = N_Q + 2 * N_KV
+PLANE_STEP = 4
+UNIT_BANKS = 2
+
+FLOPS = 2 * ROWS * K * N_ALL
+
+
+def tile_groupedqueryattention_pa_kernel(
+    tc, x, w_q_words, w_q_scales, w_k_words, w_k_scales, w_v_words, w_v_scales, cos_tab, sin_tab,
+    out_0, out_1, out_2,
+):
+    nc = tc.nc
+    with ExitStack() as ctx:
+        keep = ctx.enter_context(tc.tile_pool(name="keep", bufs=1))
+        stage = ctx.enter_context(tc.tile_pool(name="stage", bufs=3))
+        unit_pool = ctx.enter_context(tc.tile_pool(name="unit_pool", bufs=6))
+        psum = ctx.enter_context(tc.psum_pool(name="psum", bufs=8))
+        ctx.enter_context(tc.manual_schedule())
+
+        w_scales = keep.tile([P, N_ALL], U8, align_bytes=64)
+        nc.vector.memset(w_scales[:].bitcast(I32), 0)
+
+        ident = keep.tile([P, P], F32)
+        make_identity(nc, ident[:])
+
+        x_sb = keep.tile([P, ROW_SETS, K], BF16)
+        x_view = x.rearrange("(p j) k -> p j k", j=ROW_SETS)
+
+        def load_x(j, count):
+            nc.sync.dma_start(out=x_sb[:, j : j + count, :], in_=x_view[:, j : j + count, :])
+
+        def load_scales(scales, col, width):
+            for quadrant in range(4):
+                nc.sync.dma_start(
+                    out=w_scales[32 * quadrant : 32 * quadrant + PASSES * PLANE_STEP, col : col + width].bitcast(I32),
+                    in_=scales[:, 4 * quadrant : 4 * quadrant + 4, :].bitcast(I32),
+                )
+
+        def load_words(words, width, name):
+            tile = keep.tile([P, PASSES, width], U32, name=name, align_bytes=64)
+            for g in range(PASSES):
+                nc.sync.dma_start(
+                    out=tile[:, g, :].bitcast(I32),
+                    in_=words[g].rearrange("p n t -> p (n t)").bitcast(I32),
+                )
+            return tile
+
+        load_x(0, 1)
+        load_x(1, 1)
+        load_scales(w_k_scales, K_COL, N_KV)
+        load_x(2, 2)
+        load_x(4, 2)
+        load_x(6, 2)
+        wk = load_words(w_k_words, N_KV, "wk")
+        cos_bf = keep.tile([P, ROW_SETS, HEAD], BF16)
+        sin_bf = keep.tile([P, ROW_SETS, HEAD], BF16)
+        nc.sync.dma_start(out=cos_bf[:], in_=cos_tab.rearrange("(p j) d -> p j d", j=ROW_SETS))
+        nc.sync.dma_start(out=sin_bf[:], in_=sin_tab.rearrange("(p j) d -> p j d", j=ROW_SETS))
+        load_scales(w_v_scales, V_COL, N_KV)
+        wv = load_words(w_v_words, N_KV, "wv")
+        load_scales(w_q_scales, Q_COL, N_Q)
+        wq = load_words(w_q_words, N_Q, "wq")
+
+        x_codes = keep.tile([P, ROW_SETS, PASSES * P], U32, align_bytes=64)
+        x_scales = keep.tile([P, ROW_SETS, PASSES * P], U8, align_bytes=64)
+        for j in range(ROW_SETS):
+            x_words = x_sb[:, j, :].bitcast(F32)
+            turned = psum.tile([P, PASSES, 2, P], F32, tag="bank")
+            for g in range(PASSES):
+                for u in range(2):
+                    first = (K_PASS // 2) * g + u
+                    nc.tensor.transpose(
+                        turned[:, g, u, :], x_words[:, first : (K_PASS // 2) * (g + 1) : 2], ident[:]
+                    )
+            grouped = stage.tile([P, PASSES * P * 4], BF16, align_bytes=64)
+            nc.scalar.copy(
+                out=grouped[:].bitcast(F32).rearrange("p (g r u) -> p g r u", g=PASSES, u=2),
+                in_=turned[:].rearrange("p g u r -> p g r u"),
+            )
+            nc.vector.quantize_mx(
+                out=x_codes[:, j, :].bitcast(FP8X4), scales=x_scales[:, j, :], in_=grouped[:]
+            )
+
+        factors = keep.tile([P, ROW_SETS, 2, HEAD], F32)
+        nc.vector.tensor_copy(out=factors[:, :, 0, :], in_=cos_bf[:])
+        nc.vector.tensor_copy(out=factors[:, :, 1, 0:HALF], in_=sin_bf[:, :, HALF:HEAD])
+        nc.vector.tensor_scalar_mul(out=factors[:, :, 1, HALF:HEAD], in0=sin_bf[:, :, 0:HALF], scalar1=-1.0)
+
+        def project(j, words, first_col, scale_col):
+            acc = psum.tile([P, BANK], F32, tag="bank")
+            for g in range(PASSES):
+                nc.tensor.matmul_mx(
+                    out=acc[:],
+                    lhsT=x_codes[:, j, P * g : P * (g + 1)].bitcast(FP8X4),
+                    lhsT_scale=x_scales[:, j, P * g : P * (g + 1)],
+                    rhs=words[:, g, first_col : first_col + BANK].bitcast(FP8X4),
+                    rhs_scale=w_scales[PLANE_STEP * g : P, scale_col + first_col : scale_col + first_col + BANK],
+                    start=(g == 0),
+                    stop=(g == PASSES - 1),
+                )
+            return acc
+
+        def rotated_unit(banks):
+            products = unit_pool.tile([P, 2, UNIT_BANKS * BANK], F32)
+            for b, (j, words, first_col, scale_col) in enumerate(banks):
+                acc = project(j, words, first_col, scale_col)
+                shape = [P, 2, HEADS_PER_BANK, HEAD]
+                nc.vector.tensor_mul(
+                    out=products[:, :, BANK * b : BANK * (b + 1)].rearrange("p f (h d) -> p f h d", d=HEAD),
+                    in0=acc[:].rearrange("p (h d) -> p h d", d=HEAD).unsqueeze(1).to_broadcast(shape),
+                    in1=factors[:, j].unsqueeze(2).to_broadcast(shape),
+                )
+            straight = products[:, 0, :].rearrange("p (h a d) -> p h a d", a=2, d=HALF)
+            crossed = products[:, 1, :].rearrange("p (h a d) -> p h a d", a=2, d=HALF)
+            for half in range(2):
+                nc.gpsimd.tensor_add(
+                    out=straight[:, :, half, :], in0=straight[:, :, half, :], in1=crossed[:, :, 1 - half, :]
+                )
+            return products
+
+        k_view = out_1.rearrange("(p j) h d -> p j (h d)", j=ROW_SETS)
+        for first in range(0, ROW_SETS, UNIT_BANKS):
+            products = rotated_unit([(j, wk, 0, K_COL) for j in range(first, first + UNIT_BANKS)])
+            nc.sync.dma_start(
+                out=k_view[:, first : first + UNIT_BANKS, :],
+                in_=products[:, 0, :].rearrange("p (j n) -> p j n", n=N_KV),
+            )
+
+        v_rows = keep.tile([P, ROW_SETS, N_KV], F32)
+        v_view = out_2.rearrange("(p j) h d -> p j (h d)", j=ROW_SETS)
+        for j in range(ROW_SETS):
+            acc = project(j, wv, 0, V_COL)
+            nc.scalar.copy(out=v_rows[:, j, :], in_=acc[:])
+            if j % 2 == 1:
+                nc.sync.dma_start(out=v_view[:, j - 1 : j + 1, :], in_=v_rows[:, j - 1 : j + 1, :])
+
+        q_view = out_0.rearrange("(p j) h d -> p j (h d)", j=ROW_SETS)
+        unit_cols = UNIT_BANKS * BANK
+        for j in range(ROW_SETS):
+            for first_col in range(0, N_Q, unit_cols):
+                products = rotated_unit([(j, wq, first_col + BANK * b, Q_COL) for b in range(UNIT_BANKS)])
+                nc.sync.dma_start(out=q_view[:, j, first_col : first_col + unit_cols], in_=products[:, 0, :])

@@ -39,6 +39,7 @@ def tile_groupedqueryattention_pa_kernel(
         keep = ctx.enter_context(tc.tile_pool(name="keep", bufs=1))
         stage = ctx.enter_context(tc.tile_pool(name="stage", bufs=3))
         unit_pool = ctx.enter_context(tc.tile_pool(name="unit_pool", bufs=6))
+        result_pool = ctx.enter_context(tc.tile_pool(name="result_pool", bufs=6))
         psum = ctx.enter_context(tc.psum_pool(name="psum", bufs=8))
         ctx.enter_context(tc.manual_schedule())
 
@@ -107,9 +108,10 @@ def tile_groupedqueryattention_pa_kernel(
             )
 
         factors = keep.tile([P, ROW_SETS, 2, HEAD], F32)
-        nc.vector.tensor_copy(out=factors[:, :, 0, :], in_=cos_bf[:])
+        nc.vector.tensor_copy(out=factors[:, :, 0, 0:HALF], in_=cos_bf[:, :, 0:HALF])
+        nc.vector.tensor_scalar_mul(out=factors[:, :, 0, HALF:HEAD], in0=sin_bf[:, :, 0:HALF], scalar1=-1.0)
         nc.vector.tensor_copy(out=factors[:, :, 1, 0:HALF], in_=sin_bf[:, :, HALF:HEAD])
-        nc.vector.tensor_scalar_mul(out=factors[:, :, 1, HALF:HEAD], in0=sin_bf[:, :, 0:HALF], scalar1=-1.0)
+        nc.vector.tensor_copy(out=factors[:, :, 1, HALF:HEAD], in_=cos_bf[:, :, HALF:HEAD])
 
         def project(j, words, first_col, scale_col):
             acc = psum.tile([P, BANK], F32, tag="bank")
@@ -135,20 +137,21 @@ def tile_groupedqueryattention_pa_kernel(
                     in0=acc[:].rearrange("p (h d) -> p h d", d=HEAD).unsqueeze(1).to_broadcast(shape),
                     in1=factors[:, j].unsqueeze(2).to_broadcast(shape),
                 )
-            straight = products[:, 0, :].rearrange("p (h a d) -> p h a d", a=2, d=HALF)
-            crossed = products[:, 1, :].rearrange("p (h a d) -> p h a d", a=2, d=HALF)
-            for half in range(2):
-                nc.gpsimd.tensor_add(
-                    out=straight[:, :, half, :], in0=straight[:, :, half, :], in1=crossed[:, :, 1 - half, :]
-                )
-            return products
+            halves = products[:].rearrange("p f (h a d) -> p h f a d", a=2, d=HALF)
+            rotated = result_pool.tile([P, UNIT_BANKS * BANK], F32)
+            nc.gpsimd.tensor_add(
+                out=rotated[:].rearrange("p (h f d) -> p h f d", f=2, d=HALF),
+                in0=halves[:, :, :, 0, :],
+                in1=halves[:, :, :, 1, :],
+            )
+            return rotated
 
         k_view = out_1.rearrange("(p j) h d -> p j (h d)", j=ROW_SETS)
         for first in range(0, ROW_SETS, UNIT_BANKS):
-            products = rotated_unit([(j, wk, 0, K_COL) for j in range(first, first + UNIT_BANKS)])
+            rotated = rotated_unit([(j, wk, 0, K_COL) for j in range(first, first + UNIT_BANKS)])
             nc.sync.dma_start(
                 out=k_view[:, first : first + UNIT_BANKS, :],
-                in_=products[:, 0, :].rearrange("p (j n) -> p j n", n=N_KV),
+                in_=rotated[:].rearrange("p (j n) -> p j n", n=N_KV),
             )
 
         v_rows = keep.tile([P, ROW_SETS, N_KV], F32)
@@ -163,5 +166,5 @@ def tile_groupedqueryattention_pa_kernel(
         unit_cols = UNIT_BANKS * BANK
         for j in range(ROW_SETS):
             for first_col in range(0, N_Q, unit_cols):
-                products = rotated_unit([(j, wq, first_col + BANK * b, Q_COL) for b in range(UNIT_BANKS)])
-                nc.sync.dma_start(out=q_view[:, j, first_col : first_col + unit_cols], in_=products[:, 0, :])
+                rotated = rotated_unit([(j, wq, first_col + BANK * b, Q_COL) for b in range(UNIT_BANKS)])
+                nc.sync.dma_start(out=q_view[:, j, first_col : first_col + unit_cols], in_=rotated[:])

@@ -22,12 +22,10 @@ BANK = 512
 HEADS_PER_BANK = BANK // HEAD
 N_Q = 16 * HEAD
 N_KV = 4 * HEAD
-Q_COL, K_COL, V_COL = 0, N_Q, N_Q + N_KV
-N_ALL = N_Q + 2 * N_KV
+Q_BANKS = N_Q // BANK
 PLANE_STEP = 4
-UNIT_BANKS = 2
 
-FLOPS = 2 * ROWS * K * N_ALL
+FLOPS = 2 * ROWS * K * (N_Q + 2 * N_KV)
 
 
 def tile_groupedqueryattention_pa_kernel(
@@ -38,60 +36,89 @@ def tile_groupedqueryattention_pa_kernel(
     with ExitStack() as ctx:
         keep = ctx.enter_context(tc.tile_pool(name="keep", bufs=1))
         stage = ctx.enter_context(tc.tile_pool(name="stage", bufs=3))
-        unit_pool = ctx.enter_context(tc.tile_pool(name="unit_pool", bufs=6))
+        product_pool = ctx.enter_context(tc.tile_pool(name="product_pool", bufs=4))
         result_pool = ctx.enter_context(tc.tile_pool(name="result_pool", bufs=6))
-        psum = ctx.enter_context(tc.psum_pool(name="psum", bufs=8))
+        turn_psum = ctx.enter_context(tc.psum_pool(name="turn_psum", bufs=2))
+        rope_psum = ctx.enter_context(tc.psum_pool(name="rope_psum", bufs=5))
+        v_psum = ctx.enter_context(tc.psum_pool(name="v_psum", bufs=1))
         ctx.enter_context(tc.manual_schedule())
 
-        w_scales = keep.tile([P, N_ALL], U8, align_bytes=64)
-        nc.vector.memset(w_scales[:].bitcast(I32), 0)
+        k_scales = keep.tile([P, N_KV], U8, align_bytes=64)
+        q_scales = keep.tile([P, N_Q], U8, align_bytes=64)
+        v_scales = keep.tile([P, N_KV], U8, align_bytes=64)
+        nc.vector.memset(k_scales[:].bitcast(I32), 0)
+        nc.vector.memset(q_scales[:].bitcast(I32), 0)
+        nc.vector.memset(v_scales[:].bitcast(I32), 0)
 
         ident = keep.tile([P, P], F32)
         make_identity(nc, ident[:])
 
         x_sb = keep.tile([P, ROW_SETS, K], BF16)
         x_view = x.rearrange("(p j) k -> p j k", j=ROW_SETS)
+        cos_bf = keep.tile([P, ROW_SETS, HEAD], BF16)
+        sin_bf = keep.tile([P, ROW_SETS, HEAD], BF16)
+        cos_view = cos_tab.rearrange("(p j) d -> p j d", j=ROW_SETS)
+        sin_view = sin_tab.rearrange("(p j) d -> p j d", j=ROW_SETS)
 
         def load_x(j, count):
             nc.sync.dma_start(out=x_sb[:, j : j + count, :], in_=x_view[:, j : j + count, :])
 
-        def load_scales(scales, col, width):
+        def load_tables(j, count):
+            nc.sync.dma_start(out=cos_bf[:, j : j + count, :], in_=cos_view[:, j : j + count, :])
+            nc.sync.dma_start(out=sin_bf[:, j : j + count, :], in_=sin_view[:, j : j + count, :])
+
+        def load_scales(tile, scales):
             for quadrant in range(4):
                 nc.sync.dma_start(
-                    out=w_scales[32 * quadrant : 32 * quadrant + PASSES * PLANE_STEP, col : col + width].bitcast(I32),
+                    out=tile[32 * quadrant : 32 * quadrant + PASSES * PLANE_STEP, :].bitcast(I32),
                     in_=scales[:, 4 * quadrant : 4 * quadrant + 4, :].bitcast(I32),
                 )
 
-        def load_words(words, width, name):
-            tile = keep.tile([P, PASSES, width], U32, name=name, align_bytes=64)
+        def load_words(words, first_col, name):
+            tile = keep.tile([P, PASSES, BANK], U32, name=name, align_bytes=64)
             for g in range(PASSES):
                 nc.sync.dma_start(
                     out=tile[:, g, :].bitcast(I32),
-                    in_=words[g].rearrange("p n t -> p (n t)").bitcast(I32),
+                    in_=words[g].rearrange("p n t -> p (n t)")[:, 4 * first_col : 4 * (first_col + BANK)].bitcast(I32),
                 )
             return tile
 
         load_x(0, 1)
+        load_scales(k_scales, w_k_scales)
+        load_tables(0, 2)
         load_x(1, 1)
-        load_scales(w_k_scales, K_COL, N_KV)
+        wk = load_words(w_k_words, 0, "wk")
+        load_scales(q_scales, w_q_scales)
+        wq = [load_words(w_q_words, BANK * c, "wq%d" % c) for c in range(Q_BANKS)]
+        load_tables(2, ROW_SETS - 2)
         load_x(2, 2)
+        load_scales(v_scales, w_v_scales)
+        wv = load_words(w_v_words, 0, "wv")
         load_x(4, 2)
         load_x(6, 2)
-        wk = load_words(w_k_words, N_KV, "wk")
-        cos_bf = keep.tile([P, ROW_SETS, HEAD], BF16)
-        sin_bf = keep.tile([P, ROW_SETS, HEAD], BF16)
-        nc.sync.dma_start(out=cos_bf[:], in_=cos_tab.rearrange("(p j) d -> p j d", j=ROW_SETS))
-        nc.sync.dma_start(out=sin_bf[:], in_=sin_tab.rearrange("(p j) d -> p j d", j=ROW_SETS))
-        load_scales(w_v_scales, V_COL, N_KV)
-        wv = load_words(w_v_words, N_KV, "wv")
-        load_scales(w_q_scales, Q_COL, N_Q)
-        wq = load_words(w_q_words, N_Q, "wq")
+
+        factors = keep.tile([P, ROW_SETS, 2, HEAD], F32)
+
+        def factor_views(first, count):
+            rows = slice(first, first + count)
+            flat = factors[:, rows].rearrange("p j f d -> p j (f d)")
+            cos_out = flat.rearrange("p j (a d) -> p j a d", d=HALF)[:, :, 0:4:3, :]
+            cos_in = cos_bf[:, rows, :].rearrange("p j (a d) -> p j a d", d=HALF)
+            return (
+                (cos_out, cos_in, 1.0),
+                (flat[:, :, HALF:HEAD], sin_bf[:, rows, 0:HALF], -1.0),
+                (flat[:, :, HEAD : HEAD + HALF], sin_bf[:, rows, HALF:HEAD], 1.0),
+            )
+
+        for out_view, in_view, sign in factor_views(0, 2):
+            nc.vector.tensor_scalar_mul(out=out_view, in0=in_view, scalar1=sign)
 
         x_codes = keep.tile([P, ROW_SETS, PASSES * P], U32, align_bytes=64)
         x_scales = keep.tile([P, ROW_SETS, PASSES * P], U8, align_bytes=64)
-        for j in range(ROW_SETS):
+
+        def quantise_row_set(j):
             x_words = x_sb[:, j, :].bitcast(F32)
-            turned = psum.tile([P, PASSES, 2, P], F32, tag="bank")
+            turned = turn_psum.tile([P, PASSES, 2, P], F32)
             for g in range(PASSES):
                 for u in range(2):
                     first = (K_PASS // 2) * g + u
@@ -107,30 +134,25 @@ def tile_groupedqueryattention_pa_kernel(
                 out=x_codes[:, j, :].bitcast(FP8X4), scales=x_scales[:, j, :], in_=grouped[:]
             )
 
-        factors = keep.tile([P, ROW_SETS, 2, HEAD], F32)
-        nc.vector.tensor_copy(out=factors[:, :, 0, 0:HALF], in_=cos_bf[:, :, 0:HALF])
-        nc.vector.tensor_scalar_mul(out=factors[:, :, 0, HALF:HEAD], in0=sin_bf[:, :, 0:HALF], scalar1=-1.0)
-        nc.vector.tensor_copy(out=factors[:, :, 1, 0:HALF], in_=sin_bf[:, :, HALF:HEAD])
-        nc.vector.tensor_copy(out=factors[:, :, 1, HALF:HEAD], in_=cos_bf[:, :, HALF:HEAD])
-
-        def project(j, words, first_col, scale_col):
-            acc = psum.tile([P, BANK], F32, tag="bank")
+        def project(pool, j, words, scales, first_col):
+            acc = pool.tile([P, BANK], F32, tag="acc")
             for g in range(PASSES):
                 nc.tensor.matmul_mx(
                     out=acc[:],
                     lhsT=x_codes[:, j, P * g : P * (g + 1)].bitcast(FP8X4),
                     lhsT_scale=x_scales[:, j, P * g : P * (g + 1)],
-                    rhs=words[:, g, first_col : first_col + BANK].bitcast(FP8X4),
-                    rhs_scale=w_scales[PLANE_STEP * g : P, scale_col + first_col : scale_col + first_col + BANK],
+                    rhs=words[:, g, :].bitcast(FP8X4),
+                    rhs_scale=scales[PLANE_STEP * g : P, first_col : first_col + BANK],
                     start=(g == 0),
                     stop=(g == PASSES - 1),
                 )
             return acc
 
         def rotated_unit(banks):
-            products = unit_pool.tile([P, 2, UNIT_BANKS * BANK], F32)
-            for b, (j, words, first_col, scale_col) in enumerate(banks):
-                acc = project(j, words, first_col, scale_col)
+            width = BANK * len(banks)
+            products = product_pool.tile([P, 2, width], F32, tag="products")
+            for b, (j, words, scales, first_col) in enumerate(banks):
+                acc = project(rope_psum, j, words, scales, first_col)
                 shape = [P, 2, HEADS_PER_BANK, HEAD]
                 nc.vector.tensor_mul(
                     out=products[:, :, BANK * b : BANK * (b + 1)].rearrange("p f (h d) -> p f h d", d=HEAD),
@@ -138,7 +160,7 @@ def tile_groupedqueryattention_pa_kernel(
                     in1=factors[:, j].unsqueeze(2).to_broadcast(shape),
                 )
             halves = products[:].rearrange("p f (h a d) -> p h f a d", a=2, d=HALF)
-            rotated = result_pool.tile([P, UNIT_BANKS * BANK], F32)
+            rotated = result_pool.tile([P, width], F32, tag="rotated")
             nc.gpsimd.tensor_add(
                 out=rotated[:].rearrange("p (h f d) -> p h f d", f=2, d=HALF),
                 in0=halves[:, :, :, 0, :],
@@ -147,24 +169,48 @@ def tile_groupedqueryattention_pa_kernel(
             return rotated
 
         k_view = out_1.rearrange("(p j) h d -> p j (h d)", j=ROW_SETS)
-        for first in range(0, ROW_SETS, UNIT_BANKS):
-            rotated = rotated_unit([(j, wk, 0, K_COL) for j in range(first, first + UNIT_BANKS)])
+        v_view = out_2.rearrange("(p j) h d -> p j (h d)", j=ROW_SETS)
+        q_view = out_0.rearrange("(p j) h d -> p j (h d)", j=ROW_SETS)
+
+        def k_unit(first, count):
+            rotated = rotated_unit([(j, wk, k_scales, 0) for j in range(first, first + count)])
             nc.sync.dma_start(
-                out=k_view[:, first : first + UNIT_BANKS, :],
-                in_=rotated[:].rearrange("p (j n) -> p j n", n=N_KV),
+                out=k_view[:, first : first + count, :], in_=rotated[:].rearrange("p (j n) -> p j n", n=N_KV)
             )
 
-        v_rows = keep.tile([P, ROW_SETS, N_KV], F32)
-        v_view = out_2.rearrange("(p j) h d -> p j (h d)", j=ROW_SETS)
-        for j in range(ROW_SETS):
-            acc = project(j, wv, 0, V_COL)
-            nc.scalar.copy(out=v_rows[:, j, :], in_=acc[:])
-            if j % 2 == 1:
-                nc.sync.dma_start(out=v_view[:, j - 1 : j + 1, :], in_=v_rows[:, j - 1 : j + 1, :])
+        def q_unit(j, first_bank, count):
+            rotated = rotated_unit([(j, wq[c], q_scales, BANK * c) for c in range(first_bank, first_bank + count)])
+            nc.sync.dma_start(out=q_view[:, j, BANK * first_bank : BANK * (first_bank + count)], in_=rotated[:])
 
-        q_view = out_0.rearrange("(p j) h d -> p j (h d)", j=ROW_SETS)
-        unit_cols = UNIT_BANKS * BANK
-        for j in range(ROW_SETS):
-            for first_col in range(0, N_Q, unit_cols):
-                rotated = rotated_unit([(j, wq, first_col + BANK * b, Q_COL) for b in range(UNIT_BANKS)])
-                nc.sync.dma_start(out=q_view[:, j, first_col : first_col + unit_cols], in_=rotated[:])
+        v_rows = keep.tile([P, ROW_SETS, N_KV], F32)
+
+        def v_pair(first):
+            for j in (first, first + 1):
+                acc = project(v_psum, j, wv, v_scales, 0)
+                nc.scalar.copy(out=v_rows[:, j, :], in_=acc[:])
+            nc.sync.dma_start(out=v_view[:, first : first + 2, :], in_=v_rows[:, first : first + 2, :])
+
+        quantise_row_set(0)
+        quantise_row_set(1)
+        for first in range(0, ROW_SETS, 2):
+            last_pair = first + 2 == ROW_SETS
+            if first == 0:
+                k_unit(0, 1)
+                k_unit(1, 1)
+            else:
+                k_unit(first, 2)
+            q_unit(first, 0, 2)
+            q_unit(first, 2, 2)
+            q_unit(first + 1, 0, 2)
+            if first == 0:
+                for out_view, in_view, sign in factor_views(2, ROW_SETS - 2):
+                    nc.scalar.mul(out=out_view, in_=in_view, mul=sign)
+            if not last_pair:
+                quantise_row_set(first + 2)
+                quantise_row_set(first + 3)
+                q_unit(first + 1, 2, 2)
+                v_pair(first)
+            else:
+                v_pair(first)
+                q_unit(first + 1, 2, 1)
+                q_unit(first + 1, 3, 1)

@@ -37,10 +37,11 @@ def tile_groupedqueryattention_pa_kernel(
         keep = ctx.enter_context(tc.tile_pool(name="keep", bufs=1))
         stage = ctx.enter_context(tc.tile_pool(name="stage", bufs=3))
         product_pool = ctx.enter_context(tc.tile_pool(name="product_pool", bufs=4))
+        turned_pool = ctx.enter_context(tc.tile_pool(name="turned_pool", bufs=3))
         result_pool = ctx.enter_context(tc.tile_pool(name="result_pool", bufs=6))
         turn_psum = ctx.enter_context(tc.psum_pool(name="turn_psum", bufs=2))
-        rope_psum = ctx.enter_context(tc.psum_pool(name="rope_psum", bufs=5))
-        v_psum = ctx.enter_context(tc.psum_pool(name="v_psum", bufs=1))
+        rope_psum = ctx.enter_context(tc.psum_pool(name="rope_psum", bufs=4))
+        scalar_psum = ctx.enter_context(tc.psum_pool(name="scalar_psum", bufs=2))
         ctx.enter_context(tc.manual_schedule())
 
         k_scales = keep.tile([P, N_KV], U8, align_bytes=64)
@@ -52,6 +53,9 @@ def tile_groupedqueryattention_pa_kernel(
 
         ident = keep.tile([P, P], F32)
         make_identity(nc, ident[:])
+        swap = keep.tile([P, P], F32)
+        nc.vector.tensor_copy(out=swap[:, 0:HALF], in_=ident[:, HALF:HEAD])
+        nc.vector.tensor_copy(out=swap[:, HALF:HEAD], in_=ident[:, 0:HALF])
 
         x_sb = keep.tile([P, ROW_SETS, K], BF16)
         x_view = x.rearrange("(p j) k -> p j k", j=ROW_SETS)
@@ -84,14 +88,15 @@ def tile_groupedqueryattention_pa_kernel(
             return tile
 
         load_x(0, 1)
-        load_scales(k_scales, w_k_scales)
-        load_tables(0, 2)
-        load_x(1, 1)
-        wk = load_words(w_k_words, 0, "wk")
         load_scales(q_scales, w_q_scales)
-        wq = [load_words(w_q_words, BANK * c, "wq%d" % c) for c in range(Q_BANKS)]
-        load_tables(2, ROW_SETS - 2)
+        load_tables(0, 2)
+        wq = [load_words(w_q_words, BANK * c, "wq%d" % c) for c in range(2)]
+        load_x(1, 1)
+        wq.extend([load_words(w_q_words, BANK * c, "wq%d" % c) for c in range(2, Q_BANKS)])
         load_x(2, 2)
+        load_tables(2, ROW_SETS - 2)
+        load_scales(k_scales, w_k_scales)
+        wk = load_words(w_k_words, 0, "wk")
         load_scales(v_scales, w_v_scales)
         wv = load_words(w_v_words, 0, "wv")
         load_x(4, 2)
@@ -113,12 +118,28 @@ def tile_groupedqueryattention_pa_kernel(
         for out_view, in_view, sign in factor_views(0, 2):
             nc.vector.tensor_scalar_mul(out=out_view, in0=in_view, scalar1=sign)
 
+        row_factors = keep.tile([P, ROW_SETS, 2, HEAD], F32)
+        turned_factors = keep.tile([P, ROW_SETS, 2, P], F32)
+
+        def make_row_factors(first, count):
+            rows = slice(first, first + count)
+            nc.scalar.copy(out=row_factors[:, rows, 0, :], in_=cos_bf[:, rows, :])
+            nc.scalar.copy(out=row_factors[:, rows, 1, 0:HALF], in_=sin_bf[:, rows, HALF:HEAD])
+            nc.scalar.mul(out=row_factors[:, rows, 1, HALF:HEAD], in_=sin_bf[:, rows, 0:HALF], mul=-1.0)
+
+        def turn_factors(first):
+            turned = turn_psum.tile([P, 2, 2, P], F32, tag="turned")
+            for a in range(2):
+                for plane in range(2):
+                    nc.tensor.transpose(turned[:, a, plane, :], row_factors[:, first + a, plane, :], ident[:])
+            nc.scalar.copy(out=turned_factors[:, first : first + 2], in_=turned[:])
+
         x_codes = keep.tile([P, ROW_SETS, PASSES * P], U32, align_bytes=64)
         x_scales = keep.tile([P, ROW_SETS, PASSES * P], U8, align_bytes=64)
 
         def quantise_row_set(j):
             x_words = x_sb[:, j, :].bitcast(F32)
-            turned = turn_psum.tile([P, PASSES, 2, P], F32)
+            turned = turn_psum.tile([P, PASSES, 2, P], F32, tag="turned")
             for g in range(PASSES):
                 for u in range(2):
                     first = (K_PASS // 2) * g + u
@@ -148,17 +169,20 @@ def tile_groupedqueryattention_pa_kernel(
                 )
             return acc
 
+        def multiply(out_planes, acc, both_factors):
+            shape = [P, 2, HEADS_PER_BANK, HEAD]
+            nc.vector.tensor_mul(
+                out=out_planes.rearrange("p f (h d) -> p f h d", d=HEAD),
+                in0=acc[:].rearrange("p (h d) -> p h d", d=HEAD).unsqueeze(1).to_broadcast(shape),
+                in1=both_factors.unsqueeze(2).to_broadcast(shape),
+            )
+
         def rotated_unit(banks):
             width = BANK * len(banks)
             products = product_pool.tile([P, 2, width], F32, tag="products")
             for b, (j, words, scales, first_col) in enumerate(banks):
                 acc = project(rope_psum, j, words, scales, first_col)
-                shape = [P, 2, HEADS_PER_BANK, HEAD]
-                nc.vector.tensor_mul(
-                    out=products[:, :, BANK * b : BANK * (b + 1)].rearrange("p f (h d) -> p f h d", d=HEAD),
-                    in0=acc[:].rearrange("p (h d) -> p h d", d=HEAD).unsqueeze(1).to_broadcast(shape),
-                    in1=factors[:, j].unsqueeze(2).to_broadcast(shape),
-                )
+                multiply(products[:, :, BANK * b : BANK * (b + 1)], acc, factors[:, j])
             halves = products[:].rearrange("p f (h a d) -> p h f a d", a=2, d=HALF)
             rotated = result_pool.tile([P, width], F32, tag="rotated")
             nc.gpsimd.tensor_add(
@@ -172,11 +196,39 @@ def tile_groupedqueryattention_pa_kernel(
         v_view = out_2.rearrange("(p j) h d -> p j (h d)", j=ROW_SETS)
         q_view = out_0.rearrange("(p j) h d -> p j (h d)", j=ROW_SETS)
 
-        def k_unit(first, count):
-            rotated = rotated_unit([(j, wk, k_scales, 0) for j in range(first, first + count)])
-            nc.sync.dma_start(
-                out=k_view[:, first : first + count, :], in_=rotated[:].rearrange("p (j n) -> p j n", n=N_KV)
-            )
+        k_rows = keep.tile([P, ROW_SETS, N_KV], F32)
+
+        def k_products(j):
+            acc = rope_psum.tile([P, BANK], F32, tag="acc")
+            for h in range(HEADS_PER_BANK):
+                for g in range(PASSES):
+                    nc.tensor.matmul_mx(
+                        out=acc[:, P * h : P * (h + 1)],
+                        lhsT=wk[:, g, HEAD * h : HEAD * (h + 1)].bitcast(FP8X4),
+                        lhsT_scale=k_scales[PLANE_STEP * g : P, HEAD * h : HEAD * (h + 1)],
+                        rhs=x_codes[:, j, P * g : P * (g + 1)].bitcast(FP8X4),
+                        rhs_scale=x_scales[:, j, P * g : P * (g + 1)],
+                        start=(g == 0),
+                        stop=(g == PASSES - 1),
+                    )
+            planes = turned_pool.tile([P, 2, BANK], F32, tag="planes")
+            multiply(planes[:], acc, turned_factors[:, j])
+            return planes
+
+        def k_finish(first, planes_list):
+            for a, planes in enumerate(planes_list):
+                back = scalar_psum.tile([P, BANK], F32, tag="acc")
+                for h in range(HEADS_PER_BANK):
+                    cols = slice(HEAD * h, HEAD * (h + 1))
+                    nc.tensor.matmul(
+                        out=back[:, cols], lhsT=planes[:, 0, cols], rhs=ident[:], is_transpose=True, start=True, stop=False
+                    )
+                    nc.tensor.matmul(
+                        out=back[:, cols], lhsT=planes[:, 1, cols], rhs=swap[:], is_transpose=True, start=False, stop=True
+                    )
+                nc.scalar.copy(out=k_rows[:, first + a, :], in_=back[:])
+            rows = slice(first, first + len(planes_list))
+            nc.sync.dma_start(out=k_view[:, rows, :], in_=k_rows[:, rows, :])
 
         def q_unit(j, first_bank, count):
             rotated = rotated_unit([(j, wq[c], q_scales, BANK * c) for c in range(first_bank, first_bank + count)])
@@ -186,31 +238,44 @@ def tile_groupedqueryattention_pa_kernel(
 
         def v_pair(first):
             for j in (first, first + 1):
-                acc = project(v_psum, j, wv, v_scales, 0)
+                acc = project(scalar_psum, j, wv, v_scales, 0)
                 nc.scalar.copy(out=v_rows[:, j, :], in_=acc[:])
             nc.sync.dma_start(out=v_view[:, first : first + 2, :], in_=v_rows[:, first : first + 2, :])
 
         quantise_row_set(0)
-        quantise_row_set(1)
+        make_row_factors(0, 2)
+        waiting_planes = []
         for first in range(0, ROW_SETS, 2):
+            second = first + 1
             last_pair = first + 2 == ROW_SETS
             if first == 0:
-                k_unit(0, 1)
-                k_unit(1, 1)
+                q_unit(first, 0, 1)
+                q_unit(first, 1, 1)
+                quantise_row_set(second)
             else:
-                k_unit(first, 2)
-            q_unit(first, 0, 2)
+                q_unit(first, 0, 2)
+                k_finish(first - 2, waiting_planes)
             q_unit(first, 2, 2)
-            q_unit(first + 1, 0, 2)
-            if first == 0:
-                for out_view, in_view, sign in factor_views(2, ROW_SETS - 2):
-                    nc.scalar.mul(out=out_view, in_=in_view, mul=sign)
-            if not last_pair:
+            if last_pair:
+                v_pair(first)
+                q_unit(second, 0, 2)
+                first_planes = k_products(first)
+                q_unit(second, 2, 1)
+                second_planes = k_products(second)
+                k_finish(first, [first_planes])
+                q_unit(second, 3, 1)
+                k_finish(second, [second_planes])
+            else:
+                q_unit(second, 0, 2)
+                turn_factors(first)
                 quantise_row_set(first + 2)
                 quantise_row_set(first + 3)
-                q_unit(first + 1, 2, 2)
+                if first == 0:
+                    for out_view, in_view, sign in factor_views(2, ROW_SETS - 2):
+                        nc.scalar.mul(out=out_view, in_=in_view, mul=sign)
+                    make_row_factors(2, ROW_SETS - 2)
+                if first + 4 == ROW_SETS:
+                    turn_factors(first + 2)
+                q_unit(second, 2, 2)
                 v_pair(first)
-            else:
-                v_pair(first)
-                q_unit(first + 1, 2, 1)
-                q_unit(first + 1, 3, 1)
+                waiting_planes = [k_products(first), k_products(second)]

@@ -88,15 +88,14 @@ def tile_groupedqueryattention_pa_kernel(
             return tile
 
         load_x(0, 1)
+        load_x(1, 1)
         load_scales(q_scales, w_q_scales)
         load_tables(0, 2)
-        wq = [load_words(w_q_words, BANK * c, "wq%d" % c) for c in range(2)]
-        load_x(1, 1)
-        wq.extend([load_words(w_q_words, BANK * c, "wq%d" % c) for c in range(2, Q_BANKS)])
-        load_x(2, 2)
-        load_tables(2, ROW_SETS - 2)
+        wq = [load_words(w_q_words, BANK * c, "wq%d" % c) for c in range(Q_BANKS)]
         load_scales(k_scales, w_k_scales)
         wk = load_words(w_k_words, 0, "wk")
+        load_x(2, 2)
+        load_tables(2, ROW_SETS - 2)
         load_scales(v_scales, w_v_scales)
         wv = load_words(w_v_words, 0, "wv")
         load_x(4, 2)
@@ -137,7 +136,7 @@ def tile_groupedqueryattention_pa_kernel(
         x_codes = keep.tile([P, ROW_SETS, PASSES * P], U32, align_bytes=64)
         x_scales = keep.tile([P, ROW_SETS, PASSES * P], U8, align_bytes=64)
 
-        def quantise_row_set(j):
+        def turn_row_set(j):
             x_words = x_sb[:, j, :].bitcast(F32)
             turned = turn_psum.tile([P, PASSES, 2, P], F32, tag="turned")
             for g in range(PASSES):
@@ -151,6 +150,9 @@ def tile_groupedqueryattention_pa_kernel(
                 out=grouped[:].bitcast(F32).rearrange("p (g r u) -> p g r u", g=PASSES, u=2),
                 in_=turned[:].rearrange("p g u r -> p g r u"),
             )
+            return grouped
+
+        def quantise(j, grouped):
             nc.vector.quantize_mx(
                 out=x_codes[:, j, :].bitcast(FP8X4), scales=x_scales[:, j, :], in_=grouped[:]
             )
@@ -242,21 +244,20 @@ def tile_groupedqueryattention_pa_kernel(
                 nc.scalar.copy(out=v_rows[:, j, :], in_=acc[:])
             nc.sync.dma_start(out=v_view[:, first : first + 2, :], in_=v_rows[:, first : first + 2, :])
 
-        quantise_row_set(0)
+        for j, grouped in [(j, turn_row_set(j)) for j in range(2)]:
+            quantise(j, grouped)
         make_row_factors(0, 2)
-        waiting_planes = []
         for first in range(0, ROW_SETS, 2):
             second = first + 1
             last_pair = first + 2 == ROW_SETS
             if first == 0:
                 q_unit(first, 0, 1)
                 q_unit(first, 1, 1)
-                quantise_row_set(second)
             else:
                 q_unit(first, 0, 2)
-                k_finish(first - 2, waiting_planes)
-            q_unit(first, 2, 2)
+            turn_factors(first)
             if last_pair:
+                q_unit(first, 2, 2)
                 v_pair(first)
                 q_unit(second, 0, 2)
                 first_planes = k_products(first)
@@ -266,16 +267,17 @@ def tile_groupedqueryattention_pa_kernel(
                 q_unit(second, 3, 1)
                 k_finish(second, [second_planes])
             else:
-                q_unit(second, 0, 2)
-                turn_factors(first)
-                quantise_row_set(first + 2)
-                quantise_row_set(first + 3)
+                q_unit(first, 2, 1)
+                q_unit(first, 3, 1)
+                pair_planes = [k_products(first), k_products(second)]
+                next_pair = [(j, turn_row_set(j)) for j in (first + 2, first + 3)]
+                for j, grouped in next_pair:
+                    quantise(j, grouped)
                 if first == 0:
                     for out_view, in_view, sign in factor_views(2, ROW_SETS - 2):
                         nc.scalar.mul(out=out_view, in_=in_view, mul=sign)
-                    make_row_factors(2, ROW_SETS - 2)
-                if first + 4 == ROW_SETS:
-                    turn_factors(first + 2)
+                q_unit(second, 0, 2)
+                k_finish(first, pair_planes)
                 q_unit(second, 2, 2)
                 v_pair(first)
-                waiting_planes = [k_products(first), k_products(second)]
+                make_row_factors(first + 2, 2)

@@ -37,7 +37,7 @@ def tile_groupedqueryattention_pa_kernel(
         keep = ctx.enter_context(tc.tile_pool(name="keep", bufs=1))
         stage = ctx.enter_context(tc.tile_pool(name="stage", bufs=3))
         product_pool = ctx.enter_context(tc.tile_pool(name="product_pool", bufs=4))
-        turned_pool = ctx.enter_context(tc.tile_pool(name="turned_pool", bufs=3))
+        turned_pool = ctx.enter_context(tc.tile_pool(name="turned_pool", bufs=4))
         result_pool = ctx.enter_context(tc.tile_pool(name="result_pool", bufs=6))
         turn_psum = ctx.enter_context(tc.psum_pool(name="turn_psum", bufs=2))
         rope_psum = ctx.enter_context(tc.psum_pool(name="rope_psum", bufs=4))
@@ -92,9 +92,9 @@ def tile_groupedqueryattention_pa_kernel(
         load_scales(q_scales, w_q_scales)
         load_tables(0, 2)
         wq = [load_words(w_q_words, BANK * c, "wq%d" % c) for c in range(Q_BANKS)]
+        load_x(2, 2)
         load_scales(k_scales, w_k_scales)
         wk = load_words(w_k_words, 0, "wk")
-        load_x(2, 2)
         load_tables(2, ROW_SETS - 2)
         load_scales(v_scales, w_v_scales)
         wv = load_words(w_v_words, 0, "wv")
@@ -236,6 +236,13 @@ def tile_groupedqueryattention_pa_kernel(
             rotated = rotated_unit([(j, wq[c], q_scales, BANK * c) for c in range(first_bank, first_bank + count)])
             nc.sync.dma_start(out=q_view[:, j, BANK * first_bank : BANK * (first_bank + count)], in_=rotated[:])
 
+        def q_column_unit(first, count, c):
+            rotated = rotated_unit([(j, wq[c], q_scales, BANK * c) for j in range(first, first + count)])
+            nc.sync.dma_start(
+                out=q_view[:, first : first + count, BANK * c : BANK * (c + 1)],
+                in_=rotated[:].rearrange("p (j n) -> p j n", n=BANK),
+            )
+
         v_rows = keep.tile([P, ROW_SETS, N_KV], F32)
 
         def v_pair(first):
@@ -244,40 +251,56 @@ def tile_groupedqueryattention_pa_kernel(
                 nc.scalar.copy(out=v_rows[:, j, :], in_=acc[:])
             nc.sync.dma_start(out=v_view[:, first : first + 2, :], in_=v_rows[:, first : first + 2, :])
 
-        for j, grouped in [(j, turn_row_set(j)) for j in range(2)]:
-            quantise(j, grouped)
+        def make_ready(first):
+            for j, grouped in [(j, turn_row_set(j)) for j in (first, first + 1)]:
+                quantise(j, grouped)
+
+        make_ready(0)
         make_row_factors(0, 2)
-        for first in range(0, ROW_SETS, 2):
-            second = first + 1
-            last_pair = first + 2 == ROW_SETS
-            if first == 0:
-                q_unit(first, 0, 1)
-                q_unit(first, 1, 1)
-            else:
-                q_unit(first, 0, 2)
-            turn_factors(first)
-            if last_pair:
-                q_unit(first, 2, 2)
-                v_pair(first)
-                q_unit(second, 0, 2)
-                first_planes = k_products(first)
-                q_unit(second, 2, 1)
-                second_planes = k_products(second)
-                k_finish(first, [first_planes])
-                q_unit(second, 3, 1)
-                k_finish(second, [second_planes])
-            else:
-                q_unit(first, 2, 1)
-                q_unit(first, 3, 1)
-                pair_planes = [k_products(first), k_products(second)]
-                next_pair = [(j, turn_row_set(j)) for j in (first + 2, first + 3)]
-                for j, grouped in next_pair:
-                    quantise(j, grouped)
-                if first == 0:
-                    for out_view, in_view, sign in factor_views(2, ROW_SETS - 2):
-                        nc.scalar.mul(out=out_view, in_=in_view, mul=sign)
-                q_unit(second, 0, 2)
-                k_finish(first, pair_planes)
-                q_unit(second, 2, 2)
-                v_pair(first)
-                make_row_factors(first + 2, 2)
+
+        q_column_unit(0, 1, 0)
+        q_column_unit(1, 1, 0)
+        turn_factors(0)
+        for c in range(1, Q_BANKS):
+            q_column_unit(0, 2, c)
+        make_ready(2)
+        for out_view, in_view, sign in factor_views(2, ROW_SETS - 2):
+            nc.scalar.mul(out=out_view, in_=in_view, mul=sign)
+        make_row_factors(2, 2)
+        planes_before = [k_products(0), k_products(1)]
+
+        q_unit(2, 0, 2)
+        q_unit(2, 2, 2)
+        turn_factors(2)
+        pair_planes = [k_products(2), k_products(3)]
+        k_finish(0, planes_before)
+        make_ready(4)
+        q_unit(3, 0, 2)
+        k_finish(2, pair_planes)
+        q_unit(3, 2, 2)
+        v_pair(0)
+        make_row_factors(4, 2)
+
+        q_unit(4, 0, 2)
+        turn_factors(4)
+        v_pair(2)
+        q_unit(4, 2, 2)
+        pair_planes = [k_products(4), k_products(5)]
+        make_ready(6)
+        make_row_factors(6, 2)
+        q_unit(5, 0, 2)
+        k_finish(4, pair_planes)
+        turn_factors(6)
+        q_unit(5, 2, 2)
+        v_pair(4)
+
+        q_unit(6, 0, 2)
+        v_pair(6)
+        q_unit(6, 2, 2)
+        q_unit(7, 0, 2)
+        first_planes = k_products(6)
+        q_unit(7, 2, 1)
+        second_planes = k_products(7)
+        k_finish(6, [first_planes])
+        q_unit(7, 3, 1)
+        k_finish(7, [second_planes])

@@ -37,7 +37,8 @@ def tile_groupedqueryattention_pa_kernel(
         keep = ctx.enter_context(tc.tile_pool(name="keep", bufs=1))
         stage = ctx.enter_context(tc.tile_pool(name="stage", bufs=3))
         product_pool = ctx.enter_context(tc.tile_pool(name="product_pool", bufs=4))
-        turned_pool = ctx.enter_context(tc.tile_pool(name="turned_pool", bufs=4))
+        turned_pool = ctx.enter_context(tc.tile_pool(name="turned_pool", bufs=6))
+        sums_pool = ctx.enter_context(tc.tile_pool(name="sums_pool", bufs=2))
         result_pool = ctx.enter_context(tc.tile_pool(name="result_pool", bufs=6))
         turn_psum = ctx.enter_context(tc.psum_pool(name="turn_psum", bufs=2))
         rope_psum = ctx.enter_context(tc.psum_pool(name="rope_psum", bufs=4))
@@ -47,8 +48,8 @@ def tile_groupedqueryattention_pa_kernel(
         k_scales = keep.tile([P, N_KV], U8, align_bytes=64)
         q_scales = keep.tile([P, N_Q], U8, align_bytes=64)
         v_scales = keep.tile([P, N_KV], U8, align_bytes=64)
-        nc.vector.memset(k_scales[:].bitcast(I32), 0)
         nc.vector.memset(q_scales[:].bitcast(I32), 0)
+        nc.vector.memset(k_scales[:].bitcast(I32), 0)
         nc.vector.memset(v_scales[:].bitcast(I32), 0)
 
         ident = keep.tile([P, P], F32)
@@ -80,26 +81,24 @@ def tile_groupedqueryattention_pa_kernel(
 
         def load_words(words, first_col, name):
             tile = keep.tile([P, PASSES, BANK], U32, name=name, align_bytes=64)
-            for g in range(PASSES):
-                nc.sync.dma_start(
-                    out=tile[:, g, :].bitcast(I32),
-                    in_=words[g].rearrange("p n t -> p (n t)")[:, 4 * first_col : 4 * (first_col + BANK)].bitcast(I32),
-                )
+            nc.sync.dma_start(
+                out=tile[:].bitcast(I32),
+                in_=words.rearrange("g p n t -> p g (n t)")[:, :, 4 * first_col : 4 * (first_col + BANK)].bitcast(I32),
+            )
             return tile
 
-        load_x(0, 1)
-        load_x(1, 1)
-        load_scales(q_scales, w_q_scales)
+        load_x(0, 2)
         load_tables(0, 2)
+        load_scales(q_scales, w_q_scales)
         wq = [load_words(w_q_words, BANK * c, "wq%d" % c) for c in range(Q_BANKS)]
         load_x(2, 2)
-        load_scales(k_scales, w_k_scales)
         wk = load_words(w_k_words, 0, "wk")
+        load_scales(k_scales, w_k_scales)
         load_tables(2, ROW_SETS - 2)
-        load_scales(v_scales, w_v_scales)
         wv = load_words(w_v_words, 0, "wv")
         load_x(4, 2)
         load_x(6, 2)
+        load_scales(v_scales, w_v_scales)
 
         factors = keep.tile([P, ROW_SETS, 2, HEAD], F32)
 
@@ -171,11 +170,11 @@ def tile_groupedqueryattention_pa_kernel(
                 )
             return acc
 
-        def multiply(out_planes, acc, both_factors):
-            shape = [P, 2, HEADS_PER_BANK, HEAD]
-            nc.vector.tensor_mul(
+        def multiply(engine, out_planes, sums, both_factors):
+            shape = [P, 2, sums.shape[1] // HEAD, HEAD]
+            engine.tensor_mul(
                 out=out_planes.rearrange("p f (h d) -> p f h d", d=HEAD),
-                in0=acc[:].rearrange("p (h d) -> p h d", d=HEAD).unsqueeze(1).to_broadcast(shape),
+                in0=sums.rearrange("p (h d) -> p h d", d=HEAD).unsqueeze(1).to_broadcast(shape),
                 in1=both_factors.unsqueeze(2).to_broadcast(shape),
             )
 
@@ -184,7 +183,10 @@ def tile_groupedqueryattention_pa_kernel(
             products = product_pool.tile([P, 2, width], F32, tag="products")
             for b, (j, words, scales, first_col) in enumerate(banks):
                 acc = project(rope_psum, j, words, scales, first_col)
-                multiply(products[:, :, BANK * b : BANK * (b + 1)], acc, factors[:, j])
+                multiply(nc.vector, products[:, :, BANK * b : BANK * (b + 1)], acc[:], factors[:, j])
+            return add_halves(products, width)
+
+        def add_halves(products, width):
             halves = products[:].rearrange("p f (h a d) -> p h f a d", a=2, d=HALF)
             rotated = result_pool.tile([P, width], F32, tag="rotated")
             nc.gpsimd.tensor_add(
@@ -200,8 +202,8 @@ def tile_groupedqueryattention_pa_kernel(
 
         k_rows = keep.tile([P, ROW_SETS, N_KV], F32)
 
-        def k_products(j):
-            acc = rope_psum.tile([P, BANK], F32, tag="acc")
+        def k_products(j, by_gpsimd):
+            acc = (scalar_psum if by_gpsimd else rope_psum).tile([P, BANK], F32, tag="acc")
             for h in range(HEADS_PER_BANK):
                 for g in range(PASSES):
                     nc.tensor.matmul_mx(
@@ -214,7 +216,12 @@ def tile_groupedqueryattention_pa_kernel(
                         stop=(g == PASSES - 1),
                     )
             planes = turned_pool.tile([P, 2, BANK], F32, tag="planes")
-            multiply(planes[:], acc, turned_factors[:, j])
+            if by_gpsimd:
+                sums = sums_pool.tile([P, BANK], F32, tag="sums")
+                nc.scalar.copy(out=sums[:], in_=acc[:])
+                multiply(nc.gpsimd, planes[:], sums[:], turned_factors[:, j])
+            else:
+                multiply(nc.vector, planes[:], acc[:], turned_factors[:, j])
             return planes
 
         def k_finish(first, planes_list):
@@ -267,40 +274,54 @@ def tile_groupedqueryattention_pa_kernel(
         for out_view, in_view, sign in factor_views(2, ROW_SETS - 2):
             nc.scalar.mul(out=out_view, in_=in_view, mul=sign)
         make_row_factors(2, 2)
-        planes_before = [k_products(0), k_products(1)]
+        planes = {}
+        planes[1] = k_products(1, True)
+        planes[0] = k_products(0, False)
 
         q_unit(2, 0, 2)
         q_unit(2, 2, 2)
         turn_factors(2)
-        pair_planes = [k_products(2), k_products(3)]
-        k_finish(0, planes_before)
+        planes[3] = k_products(3, True)
+        planes[2] = k_products(2, False)
+        k_finish(0, [planes[0], planes[1]])
         make_ready(4)
         q_unit(3, 0, 2)
-        k_finish(2, pair_planes)
         q_unit(3, 2, 2)
         v_pair(0)
         make_row_factors(4, 2)
 
         q_unit(4, 0, 2)
         turn_factors(4)
-        v_pair(2)
+        k_finish(2, [planes[2], planes[3]])
         q_unit(4, 2, 2)
-        pair_planes = [k_products(4), k_products(5)]
+        v_pair(2)
+        planes[4] = k_products(4, False)
+        planes[5] = k_products(5, False)
         make_ready(6)
         make_row_factors(6, 2)
         q_unit(5, 0, 2)
-        k_finish(4, pair_planes)
         turn_factors(6)
         q_unit(5, 2, 2)
         v_pair(4)
 
         q_unit(6, 0, 2)
-        v_pair(6)
+        k_finish(4, [planes[4], planes[5]])
         q_unit(6, 2, 2)
+        v_pair(6)
         q_unit(7, 0, 2)
-        first_planes = k_products(6)
+        planes[6] = k_products(6, False)
         q_unit(7, 2, 1)
-        second_planes = k_products(7)
-        k_finish(6, [first_planes])
-        q_unit(7, 3, 1)
-        k_finish(7, [second_planes])
+        planes[7] = k_products(7, False)
+        k_finish(6, [planes[6]])
+        last_col = BANK * (Q_BANKS - 1)
+        acc = project(rope_psum, 7, wq[Q_BANKS - 1], q_scales, last_col)
+        for part in range(2):
+            part_cols = slice(BANK // 2 * part, BANK // 2 * (part + 1))
+            products = product_pool.tile([P, 2, BANK // 2], F32, tag="products")
+            multiply(nc.vector, products[:], acc[:, part_cols], factors[:, 7])
+            rotated = add_halves(products, BANK // 2)
+            nc.sync.dma_start(
+                out=q_view[:, 7, last_col + part_cols.start : last_col + part_cols.stop], in_=rotated[:]
+            )
+            if part == 0:
+                k_finish(7, [planes[7]])

@@ -48,8 +48,8 @@ def tile_groupedqueryattention_pa_kernel(
         k_scales = keep.tile([P, N_KV], U8, align_bytes=64)
         q_scales = keep.tile([P, N_Q], U8, align_bytes=64)
         v_scales = keep.tile([P, N_KV], U8, align_bytes=64)
-        nc.vector.memset(q_scales[:].bitcast(I32), 0)
         nc.vector.memset(k_scales[:].bitcast(I32), 0)
+        nc.vector.memset(q_scales[:].bitcast(I32), 0)
         nc.vector.memset(v_scales[:].bitcast(I32), 0)
 
         ident = keep.tile([P, P], F32)
@@ -81,24 +81,26 @@ def tile_groupedqueryattention_pa_kernel(
 
         def load_words(words, first_col, name):
             tile = keep.tile([P, PASSES, BANK], U32, name=name, align_bytes=64)
-            nc.sync.dma_start(
-                out=tile[:].bitcast(I32),
-                in_=words.rearrange("g p n t -> p g (n t)")[:, :, 4 * first_col : 4 * (first_col + BANK)].bitcast(I32),
-            )
+            for g in range(PASSES):
+                nc.sync.dma_start(
+                    out=tile[:, g, :].bitcast(I32),
+                    in_=words[g].rearrange("p n t -> p (n t)")[:, 4 * first_col : 4 * (first_col + BANK)].bitcast(I32),
+                )
             return tile
 
-        load_x(0, 2)
-        load_tables(0, 2)
+        load_x(0, 1)
+        load_x(1, 1)
         load_scales(q_scales, w_q_scales)
+        load_tables(0, 2)
         wq = [load_words(w_q_words, BANK * c, "wq%d" % c) for c in range(Q_BANKS)]
         load_x(2, 2)
-        wk = load_words(w_k_words, 0, "wk")
         load_scales(k_scales, w_k_scales)
+        wk = load_words(w_k_words, 0, "wk")
         load_tables(2, ROW_SETS - 2)
+        load_scales(v_scales, w_v_scales)
         wv = load_words(w_v_words, 0, "wv")
         load_x(4, 2)
         load_x(6, 2)
-        load_scales(v_scales, w_v_scales)
 
         factors = keep.tile([P, ROW_SETS, 2, HEAD], F32)
 

@@ -37,8 +37,7 @@ def tile_groupedqueryattention_pa_kernel(
         keep = ctx.enter_context(tc.tile_pool(name="keep", bufs=1))
         stage = ctx.enter_context(tc.tile_pool(name="stage", bufs=3))
         product_pool = ctx.enter_context(tc.tile_pool(name="product_pool", bufs=4))
-        turned_pool = ctx.enter_context(tc.tile_pool(name="turned_pool", bufs=6))
-        sums_pool = ctx.enter_context(tc.tile_pool(name="sums_pool", bufs=2))
+        turned_pool = ctx.enter_context(tc.tile_pool(name="turned_pool", bufs=4))
         result_pool = ctx.enter_context(tc.tile_pool(name="result_pool", bufs=6))
         turn_psum = ctx.enter_context(tc.psum_pool(name="turn_psum", bufs=2))
         rope_psum = ctx.enter_context(tc.psum_pool(name="rope_psum", bufs=4))
@@ -127,12 +126,12 @@ def tile_groupedqueryattention_pa_kernel(
             nc.scalar.copy(out=row_factors[:, rows, 1, 0:HALF], in_=sin_bf[:, rows, HALF:HEAD])
             nc.scalar.mul(out=row_factors[:, rows, 1, HALF:HEAD], in_=sin_bf[:, rows, 0:HALF], mul=-1.0)
 
-        def turn_factors(first):
+        def turn_factors(first, count):
             turned = turn_psum.tile([P, 2, 2, P], F32, tag="turned")
-            for a in range(2):
+            for a in range(count):
                 for plane in range(2):
                     nc.tensor.transpose(turned[:, a, plane, :], row_factors[:, first + a, plane, :], ident[:])
-            nc.scalar.copy(out=turned_factors[:, first : first + 2], in_=turned[:])
+            nc.scalar.copy(out=turned_factors[:, first : first + count], in_=turned[:, 0:count])
 
         x_codes = keep.tile([P, ROW_SETS, PASSES * P], U32, align_bytes=64)
         x_scales = keep.tile([P, ROW_SETS, PASSES * P], U8, align_bytes=64)
@@ -204,8 +203,8 @@ def tile_groupedqueryattention_pa_kernel(
 
         k_rows = keep.tile([P, ROW_SETS, N_KV], F32)
 
-        def k_products(j, by_gpsimd):
-            acc = (scalar_psum if by_gpsimd else rope_psum).tile([P, BANK], F32, tag="acc")
+        def k_products(j):
+            acc = rope_psum.tile([P, BANK], F32, tag="acc")
             for h in range(HEADS_PER_BANK):
                 for g in range(PASSES):
                     nc.tensor.matmul_mx(
@@ -218,13 +217,12 @@ def tile_groupedqueryattention_pa_kernel(
                         stop=(g == PASSES - 1),
                     )
             planes = turned_pool.tile([P, 2, BANK], F32, tag="planes")
-            if by_gpsimd:
-                sums = sums_pool.tile([P, BANK], F32, tag="sums")
-                nc.scalar.copy(out=sums[:], in_=acc[:])
-                multiply(nc.gpsimd, planes[:], sums[:], turned_factors[:, j])
-            else:
-                multiply(nc.vector, planes[:], acc[:], turned_factors[:, j])
+            multiply(nc.vector, planes[:], acc[:], turned_factors[:, j])
             return planes
+
+        def k_in_rows(j):
+            rotated = rotated_unit([(j, wk, k_scales, 0)])
+            nc.sync.dma_start(out=k_view[:, j, :], in_=rotated[:])
 
         def k_finish(first, planes_list):
             for a, planes in enumerate(planes_list):
@@ -265,55 +263,55 @@ def tile_groupedqueryattention_pa_kernel(
                 quantise(j, grouped)
 
         make_ready(0)
-        make_row_factors(0, 2)
+        make_row_factors(0, 1)
 
         q_column_unit(0, 1, 0)
         q_column_unit(1, 1, 0)
-        turn_factors(0)
+        turn_factors(0, 1)
         for c in range(1, Q_BANKS):
             q_column_unit(0, 2, c)
         make_ready(2)
         for out_view, in_view, sign in factor_views(2, ROW_SETS - 2):
             nc.scalar.mul(out=out_view, in_=in_view, mul=sign)
-        make_row_factors(2, 2)
+        make_row_factors(2, 1)
         planes = {}
-        planes[1] = k_products(1, True)
-        planes[0] = k_products(0, False)
+        planes[0] = k_products(0)
+        k_in_rows(1)
 
         q_unit(2, 0, 2)
         q_unit(2, 2, 2)
-        turn_factors(2)
-        planes[3] = k_products(3, True)
-        planes[2] = k_products(2, False)
-        k_finish(0, [planes[0], planes[1]])
+        turn_factors(2, 1)
+        planes[2] = k_products(2)
+        k_in_rows(3)
+        k_finish(0, [planes[0]])
         make_ready(4)
         q_unit(3, 0, 2)
         q_unit(3, 2, 2)
         v_pair(0)
-        make_row_factors(4, 2)
+        make_row_factors(4, 1)
 
         q_unit(4, 0, 2)
-        turn_factors(4)
-        k_finish(2, [planes[2], planes[3]])
+        turn_factors(4, 1)
+        k_finish(2, [planes[2]])
         q_unit(4, 2, 2)
         v_pair(2)
-        planes[4] = k_products(4, False)
-        planes[5] = k_products(5, False)
+        planes[4] = k_products(4)
+        k_in_rows(5)
         make_ready(6)
         make_row_factors(6, 2)
         q_unit(5, 0, 2)
-        turn_factors(6)
+        turn_factors(6, 2)
         q_unit(5, 2, 2)
         v_pair(4)
 
         q_unit(6, 0, 2)
-        k_finish(4, [planes[4], planes[5]])
+        k_finish(4, [planes[4]])
         q_unit(6, 2, 2)
         v_pair(6)
         q_unit(7, 0, 2)
-        planes[6] = k_products(6, False)
+        planes[6] = k_products(6)
         q_unit(7, 2, 1)
-        planes[7] = k_products(7, False)
+        planes[7] = k_products(7)
         k_finish(6, [planes[6]])
         last_col = BANK * (Q_BANKS - 1)
         acc = project(rope_psum, 7, wq[Q_BANKS - 1], q_scales, last_col)

@@ -36,12 +36,11 @@ def tile_groupedqueryattention_pa_kernel(
     with ExitStack() as ctx:
         keep = ctx.enter_context(tc.tile_pool(name="keep", bufs=1))
         stage = ctx.enter_context(tc.tile_pool(name="stage", bufs=3))
-        product_pool = ctx.enter_context(tc.tile_pool(name="product_pool", bufs=4))
+        product_pool = ctx.enter_context(tc.tile_pool(name="product_pool", bufs=5))
         turned_pool = ctx.enter_context(tc.tile_pool(name="turned_pool", bufs=4))
-        result_pool = ctx.enter_context(tc.tile_pool(name="result_pool", bufs=6))
-        turn_psum = ctx.enter_context(tc.psum_pool(name="turn_psum", bufs=2))
-        rope_psum = ctx.enter_context(tc.psum_pool(name="rope_psum", bufs=4))
-        scalar_psum = ctx.enter_context(tc.psum_pool(name="scalar_psum", bufs=2))
+        result_pool = ctx.enter_context(tc.tile_pool(name="result_pool", bufs=5))
+        aux_psum = ctx.enter_context(tc.psum_pool(name="aux_psum", bufs=3))
+        rope_psum = ctx.enter_context(tc.psum_pool(name="rope_psum", bufs=5))
         ctx.enter_context(tc.manual_schedule())
 
         k_scales = keep.tile([P, N_KV], U8, align_bytes=64)
@@ -53,6 +52,8 @@ def tile_groupedqueryattention_pa_kernel(
 
         ident = keep.tile([P, P], F32)
         make_identity(nc, ident[:])
+        ident_bf = keep.tile([P, P], BF16)
+        nc.vector.tensor_copy(out=ident_bf[:], in_=ident[:])
         swap = keep.tile([P, P], F32)
         nc.vector.tensor_copy(out=swap[:, 0:HALF], in_=ident[:, HALF:HEAD])
         nc.vector.tensor_copy(out=swap[:, HALF:HEAD], in_=ident[:, 0:HALF])
@@ -87,58 +88,63 @@ def tile_groupedqueryattention_pa_kernel(
                 )
             return tile
 
+        half_sets = ROW_SETS // 2
         load_x(0, 1)
-        load_x(1, 1)
         load_scales(q_scales, w_q_scales)
-        load_tables(0, 2)
-        wq = [load_words(w_q_words, BANK * c, "wq%d" % c) for c in range(Q_BANKS)]
-        load_x(2, 2)
+        load_tables(0, half_sets)
+        load_x(1, 1)
+        wq = [load_words(w_q_words, 0, "wq0")]
+        for j in range(2, ROW_SETS):
+            load_x(j, 1)
+        wq.extend([load_words(w_q_words, BANK * c, "wq%d" % c) for c in range(1, Q_BANKS)])
+        load_tables(half_sets, half_sets)
         load_scales(k_scales, w_k_scales)
         wk = load_words(w_k_words, 0, "wk")
-        load_tables(2, ROW_SETS - 2)
         load_scales(v_scales, w_v_scales)
         wv = load_words(w_v_words, 0, "wv")
-        load_x(4, 2)
-        load_x(6, 2)
 
-        factors = keep.tile([P, ROW_SETS, 2, HEAD], F32)
+        factors = keep.tile([P, ROW_SETS, 2, HEAD], BF16)
 
-        def factor_views(first, count):
+        def make_factors(copy, negate, first, count):
             rows = slice(first, first + count)
             flat = factors[:, rows].rearrange("p j f d -> p j (f d)")
             cos_out = flat.rearrange("p j (a d) -> p j a d", d=HALF)[:, :, 0:4:3, :]
             cos_in = cos_bf[:, rows, :].rearrange("p j (a d) -> p j a d", d=HALF)
-            return (
-                (cos_out, cos_in, 1.0),
-                (flat[:, :, HALF:HEAD], sin_bf[:, rows, 0:HALF], -1.0),
-                (flat[:, :, HEAD : HEAD + HALF], sin_bf[:, rows, HALF:HEAD], 1.0),
-            )
+            copy(cos_out, cos_in)
+            negate(flat[:, :, HALF:HEAD], sin_bf[:, rows, 0:HALF])
+            copy(flat[:, :, HEAD : HEAD + HALF], sin_bf[:, rows, HALF:HEAD])
 
-        for out_view, in_view, sign in factor_views(0, 2):
-            nc.vector.tensor_scalar_mul(out=out_view, in0=in_view, scalar1=sign)
+        crossed = keep.tile([P, ROW_SETS, HEAD], BF16)
+        turned_factors = keep.tile([P, ROW_SETS, 2, P], BF16)
 
-        row_factors = keep.tile([P, ROW_SETS, 2, HEAD], F32)
-        turned_factors = keep.tile([P, ROW_SETS, 2, P], F32)
-
-        def make_row_factors(first, count):
+        def make_crossed(copy, negate, first, count):
             rows = slice(first, first + count)
-            nc.scalar.copy(out=row_factors[:, rows, 0, :], in_=cos_bf[:, rows, :])
-            nc.scalar.copy(out=row_factors[:, rows, 1, 0:HALF], in_=sin_bf[:, rows, HALF:HEAD])
-            nc.scalar.mul(out=row_factors[:, rows, 1, HALF:HEAD], in_=sin_bf[:, rows, 0:HALF], mul=-1.0)
+            copy(crossed[:, rows, 0:HALF], sin_bf[:, rows, HALF:HEAD])
+            negate(crossed[:, rows, HALF:HEAD], sin_bf[:, rows, 0:HALF])
 
-        def turn_factors(first, count):
-            turned = turn_psum.tile([P, 2, 2, P], F32, tag="turned")
+        on_vector = (
+            lambda out, in_: nc.vector.tensor_copy(out=out, in_=in_),
+            lambda out, in_: nc.vector.tensor_scalar_mul(out=out, in0=in_, scalar1=-1.0),
+        )
+        on_scalar = (
+            lambda out, in_: nc.scalar.copy(out=out, in_=in_),
+            lambda out, in_: nc.scalar.mul(out=out, in_=in_, mul=-1.0),
+        )
+
+        def turn_factors(copy, first, count):
+            turned = aux_psum.tile([P, count, 2, P], BF16, tag="aux")
             for a in range(count):
-                for plane in range(2):
-                    nc.tensor.transpose(turned[:, a, plane, :], row_factors[:, first + a, plane, :], ident[:])
-            nc.scalar.copy(out=turned_factors[:, first : first + count], in_=turned[:, 0:count])
+                nc.tensor.transpose(turned[:, a, 0, :], cos_bf[:, first + a, :], ident_bf[:])
+                nc.tensor.transpose(turned[:, a, 1, :], crossed[:, first + a, :], ident_bf[:])
+            copy(turned_factors[:, first : first + count], turned[:])
 
         x_codes = keep.tile([P, ROW_SETS, PASSES * P], U32, align_bytes=64)
         x_scales = keep.tile([P, ROW_SETS, PASSES * P], U8, align_bytes=64)
+        grouped_of = {}
 
         def turn_row_set(j):
             x_words = x_sb[:, j, :].bitcast(F32)
-            turned = turn_psum.tile([P, PASSES, 2, P], F32, tag="turned")
+            turned = aux_psum.tile([P, PASSES, 2, P], F32, tag="aux")
             for g in range(PASSES):
                 for u in range(2):
                     first = (K_PASS // 2) * g + u
@@ -150,15 +156,15 @@ def tile_groupedqueryattention_pa_kernel(
                 out=grouped[:].bitcast(F32).rearrange("p (g r u) -> p g r u", g=PASSES, u=2),
                 in_=turned[:].rearrange("p g u r -> p g r u"),
             )
-            return grouped
+            grouped_of[j] = grouped
 
-        def quantise(j, grouped):
+        def quantise(j):
             nc.vector.quantize_mx(
-                out=x_codes[:, j, :].bitcast(FP8X4), scales=x_scales[:, j, :], in_=grouped[:]
+                out=x_codes[:, j, :].bitcast(FP8X4), scales=x_scales[:, j, :], in_=grouped_of[j][:]
             )
 
-        def project(pool, j, words, scales, first_col):
-            acc = pool.tile([P, BANK], F32, tag="acc")
+        def project(pool, tag, j, words, scales, first_col):
+            acc = pool.tile([P, BANK], F32, tag=tag)
             for g in range(PASSES):
                 nc.tensor.matmul_mx(
                     out=acc[:],
@@ -171,21 +177,13 @@ def tile_groupedqueryattention_pa_kernel(
                 )
             return acc
 
-        def multiply(engine, out_planes, sums, both_factors):
+        def multiply(out_planes, sums, both_factors):
             shape = [P, 2, sums.shape[1] // HEAD, HEAD]
-            engine.tensor_mul(
+            nc.vector.tensor_mul(
                 out=out_planes.rearrange("p f (h d) -> p f h d", d=HEAD),
                 in0=sums.rearrange("p (h d) -> p h d", d=HEAD).unsqueeze(1).to_broadcast(shape),
                 in1=both_factors.unsqueeze(2).to_broadcast(shape),
             )
-
-        def rotated_unit(banks):
-            width = BANK * len(banks)
-            products = product_pool.tile([P, 2, width], F32, tag="products")
-            for b, (j, words, scales, first_col) in enumerate(banks):
-                acc = project(rope_psum, j, words, scales, first_col)
-                multiply(nc.vector, products[:, :, BANK * b : BANK * (b + 1)], acc[:], factors[:, j])
-            return add_halves(products, width)
 
         def add_halves(products, width):
             halves = products[:].rearrange("p f (h a d) -> p h f a d", a=2, d=HALF)
@@ -202,6 +200,7 @@ def tile_groupedqueryattention_pa_kernel(
         q_view = out_0.rearrange("(p j) h d -> p j (h d)", j=ROW_SETS)
 
         k_rows = keep.tile([P, ROW_SETS, N_KV], F32)
+        planes_of = {}
 
         def k_products(j):
             acc = rope_psum.tile([P, BANK], F32, tag="acc")
@@ -217,16 +216,13 @@ def tile_groupedqueryattention_pa_kernel(
                         stop=(g == PASSES - 1),
                     )
             planes = turned_pool.tile([P, 2, BANK], F32, tag="planes")
-            multiply(nc.vector, planes[:], acc[:], turned_factors[:, j])
-            return planes
+            multiply(planes[:], acc[:], turned_factors[:, j])
+            planes_of[j] = planes
 
-        def k_in_rows(j):
-            rotated = rotated_unit([(j, wk, k_scales, 0)])
-            nc.sync.dma_start(out=k_view[:, j, :], in_=rotated[:])
-
-        def k_finish(first, planes_list):
-            for a, planes in enumerate(planes_list):
-                back = scalar_psum.tile([P, BANK], F32, tag="acc")
+        def k_finish(first, count):
+            for j in range(first, first + count):
+                planes = planes_of[j]
+                back = aux_psum.tile([P, BANK], F32, tag="aux")
                 for h in range(HEADS_PER_BANK):
                     cols = slice(HEAD * h, HEAD * (h + 1))
                     nc.tensor.matmul(
@@ -235,93 +231,113 @@ def tile_groupedqueryattention_pa_kernel(
                     nc.tensor.matmul(
                         out=back[:, cols], lhsT=planes[:, 1, cols], rhs=swap[:], is_transpose=True, start=False, stop=True
                     )
-                nc.scalar.copy(out=k_rows[:, first + a, :], in_=back[:])
-            rows = slice(first, first + len(planes_list))
+                nc.scalar.copy(out=k_rows[:, j, :], in_=back[:])
+            rows = slice(first, first + count)
             nc.sync.dma_start(out=k_view[:, rows, :], in_=k_rows[:, rows, :])
 
-        def q_unit(j, first_bank, count):
-            rotated = rotated_unit([(j, wq[c], q_scales, BANK * c) for c in range(first_bank, first_bank + count)])
-            nc.sync.dma_start(out=q_view[:, j, BANK * first_bank : BANK * (first_bank + count)], in_=rotated[:])
+        def q_products(banks):
+            products = product_pool.tile([P, 2, BANK * len(banks)], F32, tag="products")
+            for b, (j, c) in enumerate(banks):
+                q_product(products, b, j, c)
+            return products
 
-        def q_column_unit(first, count, c):
-            rotated = rotated_unit([(j, wq[c], q_scales, BANK * c) for j in range(first, first + count)])
+        def q_product(products, b, j, c):
+            acc = project(rope_psum, "acc", j, wq[c], q_scales, BANK * c)
+            multiply(products[:, :, BANK * b : BANK * (b + 1)], acc[:], factors[:, j])
+
+        def q_row_unit(j, first_bank, count):
+            products = q_products([(j, c) for c in range(first_bank, first_bank + count)])
+            width = BANK * count
+            rotated = add_halves(products, width)
+            nc.sync.dma_start(out=q_view[:, j, BANK * first_bank : BANK * first_bank + width], in_=rotated[:])
+
+        def q_column_store(first, count, c, products):
+            rotated = add_halves(products, BANK * count)
             nc.sync.dma_start(
                 out=q_view[:, first : first + count, BANK * c : BANK * (c + 1)],
                 in_=rotated[:].rearrange("p (j n) -> p j n", n=BANK),
             )
 
+        def q_column_unit(first, count, c):
+            q_column_store(first, count, c, q_products([(j, c) for j in range(first, first + count)]))
+
         v_rows = keep.tile([P, ROW_SETS, N_KV], F32)
 
         def v_pair(first):
             for j in (first, first + 1):
-                acc = project(scalar_psum, j, wv, v_scales, 0)
+                acc = project(aux_psum, "aux", j, wv, v_scales, 0)
                 nc.scalar.copy(out=v_rows[:, j, :], in_=acc[:])
             nc.sync.dma_start(out=v_view[:, first : first + 2, :], in_=v_rows[:, first : first + 2, :])
 
-        def make_ready(first):
-            for j, grouped in [(j, turn_row_set(j)) for j in (first, first + 1)]:
-                quantise(j, grouped)
+        turn_row_set(0)
+        make_factors(*on_vector, 0, half_sets)
+        quantise(0)
+        turn_row_set(1)
+        early = [product_pool.tile([P, 2, 2 * BANK], F32, tag="products", name="early%d" % i) for i in range(2)]
+        quantise(1)
+        q_product(early[0], 0, 0, 0)
+        turn_row_set(2)
+        turn_row_set(3)
+        quantise(2)
+        quantise(3)
+        q_product(early[0], 1, 1, 0)
+        turn_row_set(4)
+        turn_row_set(5)
+        quantise(4)
+        quantise(5)
+        q_product(early[1], 0, 2, 0)
+        turn_row_set(6)
+        turn_row_set(7)
+        quantise(6)
+        quantise(7)
+        q_product(early[1], 1, 3, 0)
+        q_column_store(2, 2, 0, early[1])
+        q_column_store(0, 2, 0, early[0])
 
-        make_ready(0)
-        make_row_factors(0, 1)
-
-        q_column_unit(0, 1, 0)
-        q_column_unit(1, 1, 0)
-        turn_factors(0, 1)
-        for c in range(1, Q_BANKS):
-            q_column_unit(0, 2, c)
-        make_ready(2)
-        for out_view, in_view, sign in factor_views(2, ROW_SETS - 2):
-            nc.scalar.mul(out=out_view, in_=in_view, mul=sign)
-        make_row_factors(2, 1)
-        planes = {}
-        planes[0] = k_products(0)
-        k_in_rows(1)
-
-        q_unit(2, 0, 2)
-        q_unit(2, 2, 2)
-        turn_factors(2, 1)
-        planes[2] = k_products(2)
-        k_in_rows(3)
-        k_finish(0, [planes[0]])
-        make_ready(4)
-        q_unit(3, 0, 2)
-        q_unit(3, 2, 2)
+        q_column_unit(0, 2, 1)
+        make_crossed(*on_scalar, 0, half_sets)
+        make_crossed(*on_scalar, half_sets, half_sets)
+        make_factors(*on_scalar, half_sets, half_sets)
+        q_column_unit(2, 2, 1)
+        turn_factors(on_scalar[0], 0, half_sets)
+        k_products(0)
+        q_column_unit(0, 2, 2)
         v_pair(0)
-        make_row_factors(4, 1)
-
-        q_unit(4, 0, 2)
-        turn_factors(4, 1)
-        k_finish(2, [planes[2]])
-        q_unit(4, 2, 2)
+        k_products(1)
+        q_column_unit(2, 2, 2)
+        q_column_unit(0, 2, 3)
+        k_finish(0, 2)
         v_pair(2)
-        planes[4] = k_products(4)
-        k_in_rows(5)
-        make_ready(6)
-        make_row_factors(6, 2)
-        q_unit(5, 0, 2)
-        turn_factors(6, 2)
-        q_unit(5, 2, 2)
+        k_products(2)
+        q_column_unit(2, 2, 3)
+        turn_factors(on_scalar[0], half_sets, half_sets)
+        q_row_unit(4, 0, 2)
         v_pair(4)
-
-        q_unit(6, 0, 2)
-        k_finish(4, [planes[4]])
-        q_unit(6, 2, 2)
+        k_products(3)
+        q_row_unit(4, 2, 2)
+        k_finish(2, 2)
+        q_row_unit(5, 0, 2)
         v_pair(6)
-        q_unit(7, 0, 2)
-        planes[6] = k_products(6)
-        q_unit(7, 2, 1)
-        planes[7] = k_products(7)
-        k_finish(6, [planes[6]])
+        k_products(4)
+        q_row_unit(5, 2, 2)
+        q_row_unit(6, 0, 2)
+        k_finish(4, 1)
+        k_products(5)
+        q_row_unit(6, 2, 2)
+        q_row_unit(7, 0, 2)
+        k_products(6)
+        k_finish(5, 1)
+        q_row_unit(7, 2, 1)
+        k_products(7)
+        k_finish(6, 1)
         last_col = BANK * (Q_BANKS - 1)
-        acc = project(rope_psum, 7, wq[Q_BANKS - 1], q_scales, last_col)
+        acc = project(rope_psum, "acc", 7, wq[Q_BANKS - 1], q_scales, last_col)
+        k_finish(7, 1)
         for part in range(2):
             part_cols = slice(BANK // 2 * part, BANK // 2 * (part + 1))
             products = product_pool.tile([P, 2, BANK // 2], F32, tag="products")
-            multiply(nc.vector, products[:], acc[:, part_cols], factors[:, 7])
+            multiply(products[:], acc[:, part_cols], factors[:, 7])
             rotated = add_halves(products, BANK // 2)
             nc.sync.dma_start(
                 out=q_view[:, 7, last_col + part_cols.start : last_col + part_cols.stop], in_=rotated[:]
             )
-            if part == 0:
-                k_finish(7, [planes[7]])

@@ -36,8 +36,10 @@ def tile_groupedqueryattention_pa_kernel(
     with ExitStack() as ctx:
         keep = ctx.enter_context(tc.tile_pool(name="keep", bufs=1))
         stage = ctx.enter_context(tc.tile_pool(name="stage", bufs=3))
+        first_stage = ctx.enter_context(tc.tile_pool(name="first_stage", bufs=1))
         product_pool = ctx.enter_context(tc.tile_pool(name="product_pool", bufs=5))
-        turned_pool = ctx.enter_context(tc.tile_pool(name="turned_pool", bufs=4))
+        turned_pool = ctx.enter_context(tc.tile_pool(name="turned_pool", bufs=6))
+        back_pool = ctx.enter_context(tc.tile_pool(name="back_pool", bufs=2))
         result_pool = ctx.enter_context(tc.tile_pool(name="result_pool", bufs=5))
         aux_psum = ctx.enter_context(tc.psum_pool(name="aux_psum", bufs=3))
         rope_psum = ctx.enter_context(tc.psum_pool(name="rope_psum", bufs=5))
@@ -46,8 +48,10 @@ def tile_groupedqueryattention_pa_kernel(
         k_scales = keep.tile([P, N_KV], U8, align_bytes=64)
         q_scales = keep.tile([P, N_Q], U8, align_bytes=64)
         v_scales = keep.tile([P, N_KV], U8, align_bytes=64)
-        nc.vector.memset(k_scales[:].bitcast(I32), 0)
+        idle_words = keep.tile([P, BANK], BF16)
+        nc.gpsimd.memset(idle_words[:], 0.0)
         nc.vector.memset(q_scales[:].bitcast(I32), 0)
+        nc.vector.memset(k_scales[:].bitcast(I32), 0)
         nc.vector.memset(v_scales[:].bitcast(I32), 0)
 
         ident = keep.tile([P, P], F32)
@@ -57,6 +61,11 @@ def tile_groupedqueryattention_pa_kernel(
         swap = keep.tile([P, P], F32)
         nc.vector.tensor_copy(out=swap[:, 0:HALF], in_=ident[:, HALF:HEAD])
         nc.vector.tensor_copy(out=swap[:, HALF:HEAD], in_=ident[:, 0:HALF])
+
+        def keep_warm(count):
+            idle = rope_psum.tile([P, BANK], F32, tag="acc", name="idle")
+            for i in range(count):
+                nc.tensor.matmul(out=idle[:], lhsT=idle_words[:, 0:P], rhs=idle_words[:], start=True, stop=True)
 
         x_sb = keep.tile([P, ROW_SETS, K], BF16)
         x_view = x.rearrange("(p j) k -> p j k", j=ROW_SETS)
@@ -89,15 +98,22 @@ def tile_groupedqueryattention_pa_kernel(
             return tile
 
         half_sets = ROW_SETS // 2
+        wq = []
         load_x(0, 1)
-        load_scales(q_scales, w_q_scales)
-        load_tables(0, half_sets)
         load_x(1, 1)
-        wq = [load_words(w_q_words, 0, "wq0")]
-        for j in range(2, ROW_SETS):
-            load_x(j, 1)
-        wq.extend([load_words(w_q_words, BANK * c, "wq%d" % c) for c in range(1, Q_BANKS)])
-        load_tables(half_sets, half_sets)
+        load_tables(0, 4)
+        load_scales(q_scales, w_q_scales)
+        wq.append(load_words(w_q_words, 0 * BANK, "wq0"))
+        load_x(2, 1)
+        load_x(3, 1)
+        load_x(4, 1)
+        load_x(5, 1)
+        load_x(6, 1)
+        load_x(7, 1)
+        wq.append(load_words(w_q_words, 1 * BANK, "wq1"))
+        wq.append(load_words(w_q_words, 2 * BANK, "wq2"))
+        wq.append(load_words(w_q_words, 3 * BANK, "wq3"))
+        load_tables(4, 4)
         load_scales(k_scales, w_k_scales)
         wk = load_words(w_k_words, 0, "wk")
         load_scales(v_scales, w_v_scales)
@@ -151,12 +167,31 @@ def tile_groupedqueryattention_pa_kernel(
                     nc.tensor.transpose(
                         turned[:, g, u, :], x_words[:, first : (K_PASS // 2) * (g + 1) : 2], ident[:]
                     )
-            grouped = stage.tile([P, PASSES * P * 4], BF16, align_bytes=64)
+            grouped = stage.tile([P, PASSES * P * 4], BF16, tag="grouped", align_bytes=64)
             nc.scalar.copy(
                 out=grouped[:].bitcast(F32).rearrange("p (g r u) -> p g r u", g=PASSES, u=2),
                 in_=turned[:].rearrange("p g u r -> p g r u"),
             )
             grouped_of[j] = grouped
+
+        def turn_and_quantise_halves(j):
+            x_words = x_sb[:, j, :].bitcast(F32)
+            for g, engine_copy in enumerate((nc.scalar.copy, nc.vector.tensor_copy)):
+                turned = aux_psum.tile([P, 2, P], F32, tag="aux")
+                for u in range(2):
+                    first = (K_PASS // 2) * g + u
+                    nc.tensor.transpose(turned[:, u, :], x_words[:, first : (K_PASS // 2) * (g + 1) : 2], ident[:])
+                grouped = first_stage.tile([P, P * 4], BF16, name="grouped%d" % g, align_bytes=64)
+                engine_copy(
+                    out=grouped[:].bitcast(F32).rearrange("p (r u) -> p r u", u=2),
+                    in_=turned[:].rearrange("p u r -> p r u"),
+                )
+                grouped_of[g] = grouped
+            for g in range(PASSES):
+                cols = slice(P * g, P * (g + 1))
+                nc.vector.quantize_mx(
+                    out=x_codes[:, j, cols].bitcast(FP8X4), scales=x_scales[:, j, cols], in_=grouped_of[g][:]
+                )
 
         def quantise(j):
             nc.vector.quantize_mx(
@@ -177,18 +212,18 @@ def tile_groupedqueryattention_pa_kernel(
                 )
             return acc
 
-        def multiply(out_planes, sums, both_factors):
+        def multiply(engine, out_planes, sums, both_factors):
             shape = [P, 2, sums.shape[1] // HEAD, HEAD]
-            nc.vector.tensor_mul(
+            engine.tensor_mul(
                 out=out_planes.rearrange("p f (h d) -> p f h d", d=HEAD),
                 in0=sums.rearrange("p (h d) -> p h d", d=HEAD).unsqueeze(1).to_broadcast(shape),
                 in1=both_factors.unsqueeze(2).to_broadcast(shape),
             )
 
-        def add_halves(products, width):
+        def add_halves(engine, products, width):
             halves = products[:].rearrange("p f (h a d) -> p h f a d", a=2, d=HALF)
             rotated = result_pool.tile([P, width], F32, tag="rotated")
-            nc.gpsimd.tensor_add(
+            engine.tensor_add(
                 out=rotated[:].rearrange("p (h f d) -> p h f d", f=2, d=HALF),
                 in0=halves[:, :, :, 0, :],
                 in1=halves[:, :, :, 1, :],
@@ -202,38 +237,63 @@ def tile_groupedqueryattention_pa_kernel(
         k_rows = keep.tile([P, ROW_SETS, N_KV], F32)
         planes_of = {}
 
-        def k_products(j):
-            acc = rope_psum.tile([P, BANK], F32, tag="acc")
+        def turned_products(j, words, scales, first_col, on_gpsimd):
+            acc = (aux_psum if on_gpsimd else rope_psum).tile([P, BANK], F32, tag="aux" if on_gpsimd else "acc", name="acc")
             for h in range(HEADS_PER_BANK):
                 for g in range(PASSES):
                     nc.tensor.matmul_mx(
                         out=acc[:, P * h : P * (h + 1)],
-                        lhsT=wk[:, g, HEAD * h : HEAD * (h + 1)].bitcast(FP8X4),
-                        lhsT_scale=k_scales[PLANE_STEP * g : P, HEAD * h : HEAD * (h + 1)],
+                        lhsT=words[:, g, HEAD * h : HEAD * (h + 1)].bitcast(FP8X4),
+                        lhsT_scale=scales[PLANE_STEP * g : P, first_col + HEAD * h : first_col + HEAD * (h + 1)],
                         rhs=x_codes[:, j, P * g : P * (g + 1)].bitcast(FP8X4),
                         rhs_scale=x_scales[:, j, P * g : P * (g + 1)],
                         start=(g == 0),
                         stop=(g == PASSES - 1),
                     )
             planes = turned_pool.tile([P, 2, BANK], F32, tag="planes")
-            multiply(planes[:], acc[:], turned_factors[:, j])
-            planes_of[j] = planes
+            if on_gpsimd:
+                sums = stage.tile([P, BANK], F32, tag="sums")
+                nc.scalar.copy(out=sums[:], in_=acc[:])
+                multiply(nc.gpsimd, planes[:], sums[:], turned_factors[:, j])
+            else:
+                multiply(nc.vector, planes[:], acc[:], turned_factors[:, j])
+            return planes
 
-        def k_finish(first, count):
-            for j in range(first, first + count):
-                planes = planes_of[j]
-                back = aux_psum.tile([P, BANK], F32, tag="aux")
-                for h in range(HEADS_PER_BANK):
-                    cols = slice(HEAD * h, HEAD * (h + 1))
-                    nc.tensor.matmul(
-                        out=back[:, cols], lhsT=planes[:, 0, cols], rhs=ident[:], is_transpose=True, start=True, stop=False
-                    )
-                    nc.tensor.matmul(
-                        out=back[:, cols], lhsT=planes[:, 1, cols], rhs=swap[:], is_transpose=True, start=False, stop=True
-                    )
-                nc.scalar.copy(out=k_rows[:, j, :], in_=back[:])
+        def turn_back(planes, out):
+            back = aux_psum.tile([P, BANK], F32, tag="aux")
+            for h in range(HEADS_PER_BANK):
+                cols = slice(HEAD * h, HEAD * (h + 1))
+                nc.tensor.matmul(
+                    out=back[:, cols], lhsT=planes[:, 0, cols], rhs=ident[:], is_transpose=True, start=True, stop=False
+                )
+                nc.tensor.matmul(
+                    out=back[:, cols], lhsT=planes[:, 1, cols], rhs=swap[:], is_transpose=True, start=False, stop=True
+                )
+            nc.scalar.copy(out=out, in_=back[:])
+
+        def k_products(j, on_gpsimd=False):
+            planes_of[j] = turned_products(j, wk, k_scales, 0, on_gpsimd)
+
+        def k_finish(j):
+            turn_back(planes_of[j], k_rows[:, j, :])
+
+        def t_products(j, c, on_gpsimd=False):
+            planes_of[j, c] = turned_products(j, wq[c], q_scales, BANK * c, on_gpsimd)
+
+        def t_finish(j, c):
+            rotated = back_pool.tile([P, BANK], F32, tag="back")
+            turn_back(planes_of[j, c], rotated[:])
+            nc.sync.dma_start(out=q_view[:, j, BANK * c : BANK * (c + 1)], in_=rotated[:])
+
+        def k_store(first, count):
             rows = slice(first, first + count)
             nc.sync.dma_start(out=k_view[:, rows, :], in_=k_rows[:, rows, :])
+
+        waiting = []
+
+        def store_oldest():
+            out_view, rotated = waiting.pop(0)
+            nc.sync.dma_start(out=out_view, in_=rotated)
 
         def q_products(banks):
             products = product_pool.tile([P, 2, BANK * len(banks)], F32, tag="products")
@@ -243,20 +303,20 @@ def tile_groupedqueryattention_pa_kernel(
 
         def q_product(products, b, j, c):
             acc = project(rope_psum, "acc", j, wq[c], q_scales, BANK * c)
-            multiply(products[:, :, BANK * b : BANK * (b + 1)], acc[:], factors[:, j])
+            multiply(nc.vector, products[:, :, BANK * b : BANK * (b + 1)], acc[:], factors[:, j])
 
         def q_row_unit(j, first_bank, count):
             products = q_products([(j, c) for c in range(first_bank, first_bank + count)])
             width = BANK * count
-            rotated = add_halves(products, width)
-            nc.sync.dma_start(out=q_view[:, j, BANK * first_bank : BANK * first_bank + width], in_=rotated[:])
+            rotated = add_halves(nc.gpsimd, products, width)
+            waiting.append((q_view[:, j, BANK * first_bank : BANK * first_bank + width], rotated[:]))
 
         def q_column_store(first, count, c, products):
-            rotated = add_halves(products, BANK * count)
-            nc.sync.dma_start(
-                out=q_view[:, first : first + count, BANK * c : BANK * (c + 1)],
-                in_=rotated[:].rearrange("p (j n) -> p j n", n=BANK),
-            )
+            rotated = add_halves(nc.gpsimd, products, BANK * count)
+            waiting.append((
+                q_view[:, first : first + count, BANK * c : BANK * (c + 1)],
+                rotated[:].rearrange("p (j n) -> p j n", n=BANK),
+            ))
 
         def q_column_unit(first, count, c):
             q_column_store(first, count, c, q_products([(j, c) for j in range(first, first + count)]))
@@ -269,9 +329,8 @@ def tile_groupedqueryattention_pa_kernel(
                 nc.scalar.copy(out=v_rows[:, j, :], in_=acc[:])
             nc.sync.dma_start(out=v_view[:, first : first + 2, :], in_=v_rows[:, first : first + 2, :])
 
-        turn_row_set(0)
+        turn_and_quantise_halves(0)
         make_factors(*on_vector, 0, half_sets)
-        quantise(0)
         turn_row_set(1)
         early = [product_pool.tile([P, 2, 2 * BANK], F32, tag="products", name="early%d" % i) for i in range(2)]
         quantise(1)
@@ -297,47 +356,76 @@ def tile_groupedqueryattention_pa_kernel(
         q_column_unit(0, 2, 1)
         make_crossed(*on_scalar, 0, half_sets)
         make_crossed(*on_scalar, half_sets, half_sets)
-        make_factors(*on_scalar, half_sets, half_sets)
         q_column_unit(2, 2, 1)
+        store_oldest()
+        store_oldest()
         turn_factors(on_scalar[0], 0, half_sets)
-        k_products(0)
         q_column_unit(0, 2, 2)
+        store_oldest()
         v_pair(0)
-        k_products(1)
+        k_products(0)
+        store_oldest()
         q_column_unit(2, 2, 2)
+        store_oldest()
+        make_factors(*on_scalar, half_sets, half_sets)
         q_column_unit(0, 2, 3)
-        k_finish(0, 2)
         v_pair(2)
-        k_products(2)
+        k_products(1)
+        k_finish(0)
+        store_oldest()
         q_column_unit(2, 2, 3)
+        store_oldest()
         turn_factors(on_scalar[0], half_sets, half_sets)
         q_row_unit(4, 0, 2)
         v_pair(4)
-        k_products(3)
+        k_products(2)
+        k_finish(1)
+        k_store(0, 2)
+        store_oldest()
         q_row_unit(4, 2, 2)
-        k_finish(2, 2)
+        store_oldest()
         q_row_unit(5, 0, 2)
         v_pair(6)
-        k_products(4)
+        k_products(3)
+        k_finish(2)
+        store_oldest()
         q_row_unit(5, 2, 2)
+        store_oldest()
+        k_products(4)
         q_row_unit(6, 0, 2)
-        k_finish(4, 1)
+        k_finish(3)
+        k_store(2, 2)
+        store_oldest()
         k_products(5)
         q_row_unit(6, 2, 2)
-        q_row_unit(7, 0, 2)
+        k_finish(4)
+        store_oldest()
         k_products(6)
-        k_finish(5, 1)
-        q_row_unit(7, 2, 1)
+        q_row_unit(7, 0, 1)
         k_products(7)
-        k_finish(6, 1)
+        k_finish(5)
+        k_store(4, 2)
+        store_oldest()
+        q_row_unit(7, 1, 1)
+        q_row_unit(7, 2, 1)
+        store_oldest()
         last_col = BANK * (Q_BANKS - 1)
+        last_products = []
         acc = project(rope_psum, "acc", 7, wq[Q_BANKS - 1], q_scales, last_col)
-        k_finish(7, 1)
+        k_finish(6)
+        k_store(6, 1)
+        k_finish(7)
+        k_store(7, 1)
+        store_oldest()
+        store_oldest()
         for part in range(2):
             part_cols = slice(BANK // 2 * part, BANK // 2 * (part + 1))
             products = product_pool.tile([P, 2, BANK // 2], F32, tag="products")
-            multiply(products[:], acc[:, part_cols], factors[:, 7])
-            rotated = add_halves(products, BANK // 2)
+            multiply(nc.vector, products[:], acc[:, part_cols], factors[:, 7])
+            last_products.append(products)
+        for part in range(2):
+            part_cols = slice(BANK // 2 * part, BANK // 2 * (part + 1))
+            rotated = add_halves(nc.vector, last_products[part], BANK // 2)
             nc.sync.dma_start(
                 out=q_view[:, 7, last_col + part_cols.start : last_col + part_cols.stop], in_=rotated[:]
             )

@@ -295,6 +295,11 @@ def tile_groupedqueryattention_pa_kernel(
             out_view, rotated = waiting.pop(0)
             nc.sync.dma_start(out=out_view, in_=rotated)
 
+        gate_bytes = keep.tile([P, 64], U8, align_bytes=64)
+
+        def gate_gpsimd(j):
+            nc.gpsimd.tensor_copy(out=gate_bytes[:], in_=x_scales[:, j, 0:64])
+
         def q_products(banks):
             products = product_pool.tile([P, 2, BANK * len(banks)], F32, tag="products")
             for b, (j, c) in enumerate(banks):
@@ -329,10 +334,12 @@ def tile_groupedqueryattention_pa_kernel(
                 nc.scalar.copy(out=v_rows[:, j, :], in_=acc[:])
             nc.sync.dma_start(out=v_view[:, first : first + 2, :], in_=v_rows[:, first : first + 2, :])
 
-        turn_and_quantise_halves(0)
-        make_factors(*on_vector, 0, half_sets)
-        turn_row_set(1)
+        keep_warm(4)
         early = [product_pool.tile([P, 2, 2 * BANK], F32, tag="products", name="early%d" % i) for i in range(2)]
+        turn_and_quantise_halves(0)
+        make_factors(*on_vector, 0, 4)
+        turn_row_set(1)
+        keep_warm(2)
         quantise(1)
         q_product(early[0], 0, 0, 0)
         turn_row_set(2)
@@ -349,10 +356,10 @@ def tile_groupedqueryattention_pa_kernel(
         turn_row_set(7)
         quantise(6)
         quantise(7)
+        gate_gpsimd(7)
         q_product(early[1], 1, 3, 0)
-        q_column_store(2, 2, 0, early[1])
         q_column_store(0, 2, 0, early[0])
-
+        q_column_store(2, 2, 0, early[1])
         q_column_unit(0, 2, 1)
         make_crossed(*on_scalar, 0, half_sets)
         make_crossed(*on_scalar, half_sets, half_sets)
@@ -407,8 +414,7 @@ def tile_groupedqueryattention_pa_kernel(
         k_store(4, 2)
         store_oldest()
         q_row_unit(7, 1, 1)
-        q_row_unit(7, 2, 1)
-        store_oldest()
+        before_last = q_products([(7, Q_BANKS - 2)])
         last_col = BANK * (Q_BANKS - 1)
         last_products = []
         acc = project(rope_psum, "acc", 7, wq[Q_BANKS - 1], q_scales, last_col)
@@ -423,6 +429,9 @@ def tile_groupedqueryattention_pa_kernel(
             products = product_pool.tile([P, 2, BANK // 2], F32, tag="products")
             multiply(nc.vector, products[:], acc[:, part_cols], factors[:, 7])
             last_products.append(products)
+            if part == 0:
+                rotated = add_halves(nc.vector, before_last, BANK)
+                nc.sync.dma_start(out=q_view[:, 7, last_col - BANK : last_col], in_=rotated[:])
         for part in range(2):
             part_cols = slice(BANK // 2 * part, BANK // 2 * (part + 1))
             rotated = add_halves(nc.vector, last_products[part], BANK // 2)

@@ -36,7 +36,7 @@ def tile_groupedqueryattention_pa_kernel(
     with ExitStack() as ctx:
         keep = ctx.enter_context(tc.tile_pool(name="keep", bufs=1))
         stage = ctx.enter_context(tc.tile_pool(name="stage", bufs=3))
-        first_stage = ctx.enter_context(tc.tile_pool(name="first_stage", bufs=1))
+        first_stage = ctx.enter_context(tc.tile_pool(name="first_stage", bufs=2))
         product_pool = ctx.enter_context(tc.tile_pool(name="product_pool", bufs=5))
         turned_pool = ctx.enter_context(tc.tile_pool(name="turned_pool", bufs=6))
         back_pool = ctx.enter_context(tc.tile_pool(name="back_pool", bufs=2))
@@ -100,10 +100,10 @@ def tile_groupedqueryattention_pa_kernel(
         half_sets = ROW_SETS // 2
         wq = []
         load_x(0, 1)
-        load_x(1, 1)
-        load_tables(0, 4)
         load_scales(q_scales, w_q_scales)
+        load_x(1, 1)
         wq.append(load_words(w_q_words, 0 * BANK, "wq0"))
+        load_tables(0, 4)
         load_x(2, 1)
         load_x(3, 1)
         load_x(4, 1)
@@ -174,23 +174,25 @@ def tile_groupedqueryattention_pa_kernel(
             )
             grouped_of[j] = grouped
 
-        def turn_and_quantise_halves(j):
+        def turn_halves(j):
             x_words = x_sb[:, j, :].bitcast(F32)
             for g, engine_copy in enumerate((nc.scalar.copy, nc.vector.tensor_copy)):
                 turned = aux_psum.tile([P, 2, P], F32, tag="aux")
                 for u in range(2):
                     first = (K_PASS // 2) * g + u
                     nc.tensor.transpose(turned[:, u, :], x_words[:, first : (K_PASS // 2) * (g + 1) : 2], ident[:])
-                grouped = first_stage.tile([P, P * 4], BF16, name="grouped%d" % g, align_bytes=64)
+                grouped = first_stage.tile([P, P * 4], BF16, tag="half%d" % g, align_bytes=64)
                 engine_copy(
                     out=grouped[:].bitcast(F32).rearrange("p (r u) -> p r u", u=2),
                     in_=turned[:].rearrange("p u r -> p r u"),
                 )
-                grouped_of[g] = grouped
+                grouped_of[j, g] = grouped
+
+        def quantise_halves(j):
             for g in range(PASSES):
                 cols = slice(P * g, P * (g + 1))
                 nc.vector.quantize_mx(
-                    out=x_codes[:, j, cols].bitcast(FP8X4), scales=x_scales[:, j, cols], in_=grouped_of[g][:]
+                    out=x_codes[:, j, cols].bitcast(FP8X4), scales=x_scales[:, j, cols], in_=grouped_of[j, g][:]
                 )
 
         def quantise(j):
@@ -336,22 +338,23 @@ def tile_groupedqueryattention_pa_kernel(
 
         keep_warm(4)
         early = [product_pool.tile([P, 2, 2 * BANK], F32, tag="products", name="early%d" % i) for i in range(2)]
-        turn_and_quantise_halves(0)
-        make_factors(*on_vector, 0, 4)
+        turn_halves(0)
+        quantise_halves(0)
         turn_row_set(1)
-        keep_warm(2)
+        keep_warm(1)
         quantise(1)
+        make_factors(*on_vector, 0, 4)
         q_product(early[0], 0, 0, 0)
         turn_row_set(2)
         turn_row_set(3)
         quantise(2)
-        quantise(3)
         q_product(early[0], 1, 1, 0)
+        quantise(3)
         turn_row_set(4)
         turn_row_set(5)
         quantise(4)
-        quantise(5)
         q_product(early[1], 0, 2, 0)
+        quantise(5)
         turn_row_set(6)
         turn_row_set(7)
         quantise(6)

from contextlib import ExitStack

import concourse.mybir as mybir
from concourse.masks import make_identity

F32 = mybir.dt.float32
BF16 = mybir.dt.bfloat16
I32 = mybir.dt.int32
U32 = mybir.dt.uint32
U8 = mybir.dt.uint8
FP8X4 = mybir.dt.float8_e4m3fn_x4

P = 128
ROWS = 1024
K = 1024
K_PASS = 4 * P
PASSES = K // K_PASS
ROW_SETS = ROWS // P
HEAD = 128
HALF = HEAD // 2
BANK = 512
HEADS_PER_BANK = BANK // HEAD
N_Q = 16 * HEAD
N_KV = 4 * HEAD
Q_BANKS = N_Q // BANK
PLANE_STEP = 4

FLOPS = 2 * ROWS * K * (N_Q + 2 * N_KV)


def tile_groupedqueryattention_pa_kernel(
    tc, x, w_q_words, w_q_scales, w_k_words, w_k_scales, w_v_words, w_v_scales, cos_tab, sin_tab,
    out_0, out_1, out_2,
):
    nc = tc.nc
    with ExitStack() as ctx:
        keep = ctx.enter_context(tc.tile_pool(name="keep", bufs=1))
        stage = ctx.enter_context(tc.tile_pool(name="stage", bufs=3))
        first_stage = ctx.enter_context(tc.tile_pool(name="first_stage", bufs=2))
        product_pool = ctx.enter_context(tc.tile_pool(name="product_pool", bufs=5))
        turned_pool = ctx.enter_context(tc.tile_pool(name="turned_pool", bufs=6))
        back_pool = ctx.enter_context(tc.tile_pool(name="back_pool", bufs=2))
        result_pool = ctx.enter_context(tc.tile_pool(name="result_pool", bufs=5))
        aux_psum = ctx.enter_context(tc.psum_pool(name="aux_psum", bufs=3))
        rope_psum = ctx.enter_context(tc.psum_pool(name="rope_psum", bufs=5))
        ctx.enter_context(tc.manual_schedule())

        k_scales = keep.tile([P, N_KV], U8, align_bytes=64)
        q_scales = keep.tile([P, N_Q], U8, align_bytes=64)
        v_scales = keep.tile([P, N_KV], U8, align_bytes=64)
        idle_words = keep.tile([P, BANK], BF16)
        nc.gpsimd.memset(idle_words[:], 0.0)
        nc.vector.memset(q_scales[:].bitcast(I32), 0)
        nc.vector.memset(k_scales[:].bitcast(I32), 0)
        nc.vector.memset(v_scales[:].bitcast(I32), 0)

        ident = keep.tile([P, P], F32)
        make_identity(nc, ident[:])
        ident_bf = keep.tile([P, P], BF16)
        nc.vector.tensor_copy(out=ident_bf[:], in_=ident[:])
        swap = keep.tile([P, P], F32)
        nc.vector.tensor_copy(out=swap[:, 0:HALF], in_=ident[:, HALF:HEAD])
        nc.vector.tensor_copy(out=swap[:, HALF:HEAD], in_=ident[:, 0:HALF])

        def keep_warm(count):
            idle = rope_psum.tile([P, BANK], F32, tag="acc", name="idle")
            for i in range(count):
                nc.tensor.matmul(out=idle[:], lhsT=idle_words[:, 0:P], rhs=idle_words[:], start=True, stop=True)

        x_sb = keep.tile([P, ROW_SETS, K], BF16)
        x_view = x.rearrange("(p j) k -> p j k", j=ROW_SETS)
        cos_bf = keep.tile([P, ROW_SETS, HEAD], BF16)
        sin_bf = keep.tile([P, ROW_SETS, HEAD], BF16)
        cos_view = cos_tab.rearrange("(p j) d -> p j d", j=ROW_SETS)
        sin_view = sin_tab.rearrange("(p j) d -> p j d", j=ROW_SETS)

        def load_x(j, count):
            nc.sync.dma_start(out=x_sb[:, j : j + count, :], in_=x_view[:, j : j + count, :])

        def load_tables(j, count):
            nc.sync.dma_start(out=cos_bf[:, j : j + count, :], in_=cos_view[:, j : j + count, :])
            nc.sync.dma_start(out=sin_bf[:, j : j + count, :], in_=sin_view[:, j : j + count, :])

        def load_scales(tile, scales):
            for quadrant in range(4):
                nc.sync.dma_start(
                    out=tile[32 * quadrant : 32 * quadrant + PASSES * PLANE_STEP, :].bitcast(I32),
                    in_=scales[:, 4 * quadrant : 4 * quadrant + 4, :].bitcast(I32),
                )

        def load_words(words, first_col, name):
            tile = keep.tile([P, PASSES, BANK], U32, name=name, align_bytes=64)
            for g in range(PASSES):
                nc.sync.dma_start(
                    out=tile[:, g, :].bitcast(I32),
                    in_=words[g].rearrange("p n t -> p (n t)")[:, 4 * first_col : 4 * (first_col + BANK)].bitcast(I32),
                )
            return tile

        half_sets = ROW_SETS // 2
        wq = []
        load_x(0, 1)
        load_scales(q_scales, w_q_scales)
        load_x(1, 1)
        wq.append(load_words(w_q_words, 0 * BANK, "wq0"))
        load_tables(0, 4)
        load_x(2, 1)
        load_x(3, 1)
        load_x(4, 1)
        load_x(5, 1)
        load_x(6, 1)
        load_x(7, 1)
        wq.append(load_words(w_q_words, 1 * BANK, "wq1"))
        wq.append(load_words(w_q_words, 2 * BANK, "wq2"))
        wq.append(load_words(w_q_words, 3 * BANK, "wq3"))
        load_tables(4, 4)
        load_scales(k_scales, w_k_scales)
        wk = load_words(w_k_words, 0, "wk")
        load_scales(v_scales, w_v_scales)
        wv = load_words(w_v_words, 0, "wv")

        factors = keep.tile([P, ROW_SETS, 2, HEAD], BF16)

        def make_factors(copy, negate, first, count):
            rows = slice(first, first + count)
            flat = factors[:, rows].rearrange("p j f d -> p j (f d)")
            cos_out = flat.rearrange("p j (a d) -> p j a d", d=HALF)[:, :, 0:4:3, :]
            cos_in = cos_bf[:, rows, :].rearrange("p j (a d) -> p j a d", d=HALF)
            copy(cos_out, cos_in)
            negate(flat[:, :, HALF:HEAD], sin_bf[:, rows, 0:HALF])
            copy(flat[:, :, HEAD : HEAD + HALF], sin_bf[:, rows, HALF:HEAD])

        crossed = keep.tile([P, ROW_SETS, HEAD], BF16)
        turned_factors = keep.tile([P, ROW_SETS, 2, P], BF16)

        def make_crossed(copy, negate, first, count):
            rows = slice(first, first + count)
            copy(crossed[:, rows, 0:HALF], sin_bf[:, rows, HALF:HEAD])
            negate(crossed[:, rows, HALF:HEAD], sin_bf[:, rows, 0:HALF])

        on_vector = (
            lambda out, in_: nc.vector.tensor_copy(out=out, in_=in_),
            lambda out, in_: nc.vector.tensor_scalar_mul(out=out, in0=in_, scalar1=-1.0),
        )
        on_scalar = (
            lambda out, in_: nc.scalar.copy(out=out, in_=in_),
            lambda out, in_: nc.scalar.mul(out=out, in_=in_, mul=-1.0),
        )

        def turn_factors(copy, first, count):
            turned = aux_psum.tile([P, count, 2, P], BF16, tag="aux")
            for a in range(count):
                nc.tensor.transpose(turned[:, a, 0, :], cos_bf[:, first + a, :], ident_bf[:])
                nc.tensor.transpose(turned[:, a, 1, :], crossed[:, first + a, :], ident_bf[:])
            copy(turned_factors[:, first : first + count], turned[:])

        x_codes = keep.tile([P, ROW_SETS, PASSES * P], U32, align_bytes=64)
        x_scales = keep.tile([P, ROW_SETS, PASSES * P], U8, align_bytes=64)
        grouped_of = {}

        def turn_row_set(j):
            x_words = x_sb[:, j, :].bitcast(F32)
            turned = aux_psum.tile([P, PASSES, 2, P], F32, tag="aux")
            for g in range(PASSES):
                for u in range(2):
                    first = (K_PASS // 2) * g + u
                    nc.tensor.transpose(
                        turned[:, g, u, :], x_words[:, first : (K_PASS // 2) * (g + 1) : 2], ident[:]
                    )
            grouped = stage.tile([P, PASSES * P * 4], BF16, tag="grouped", align_bytes=64)
            nc.scalar.copy(
                out=grouped[:].bitcast(F32).rearrange("p (g r u) -> p g r u", g=PASSES, u=2),
                in_=turned[:].rearrange("p g u r -> p g r u"),
            )
            grouped_of[j] = grouped

        def turn_halves(j):
            x_words = x_sb[:, j, :].bitcast(F32)
            for g, engine_copy in enumerate((nc.scalar.copy, nc.vector.tensor_copy)):
                turned = aux_psum.tile([P, 2, P], F32, tag="aux")
                for u in range(2):
                    first = (K_PASS // 2) * g + u
                    nc.tensor.transpose(turned[:, u, :], x_words[:, first : (K_PASS // 2) * (g + 1) : 2], ident[:])
                grouped = first_stage.tile([P, P * 4], BF16, tag="half%d" % g, align_bytes=64)
                engine_copy(
                    out=grouped[:].bitcast(F32).rearrange("p (r u) -> p r u", u=2),
                    in_=turned[:].rearrange("p u r -> p r u"),
                )
                grouped_of[j, g] = grouped

        def quantise_halves(j):
            for g in range(PASSES):
                cols = slice(P * g, P * (g + 1))
                nc.vector.quantize_mx(
                    out=x_codes[:, j, cols].bitcast(FP8X4), scales=x_scales[:, j, cols], in_=grouped_of[j, g][:]
                )

        def quantise(j):
            nc.vector.quantize_mx(
                out=x_codes[:, j, :].bitcast(FP8X4), scales=x_scales[:, j, :], in_=grouped_of[j][:]
            )

        def project(pool, tag, j, words, scales, first_col):
            acc = pool.tile([P, BANK], F32, tag=tag)
            for g in range(PASSES):
                nc.tensor.matmul_mx(
                    out=acc[:],
                    lhsT=x_codes[:, j, P * g : P * (g + 1)].bitcast(FP8X4),
                    lhsT_scale=x_scales[:, j, P * g : P * (g + 1)],
                    rhs=words[:, g, :].bitcast(FP8X4),
                    rhs_scale=scales[PLANE_STEP * g : P, first_col : first_col + BANK],
                    start=(g == 0),
                    stop=(g == PASSES - 1),
                )
            return acc

        def multiply(engine, out_planes, sums, both_factors):
            shape = [P, 2, sums.shape[1] // HEAD, HEAD]
            engine.tensor_mul(
                out=out_planes.rearrange("p f (h d) -> p f h d", d=HEAD),
                in0=sums.rearrange("p (h d) -> p h d", d=HEAD).unsqueeze(1).to_broadcast(shape),
                in1=both_factors.unsqueeze(2).to_broadcast(shape),
            )

        def add_halves(engine, products, width):
            halves = products[:].rearrange("p f (h a d) -> p h f a d", a=2, d=HALF)
            rotated = result_pool.tile([P, width], F32, tag="rotated")
            engine.tensor_add(
                out=rotated[:].rearrange("p (h f d) -> p h f d", f=2, d=HALF),
                in0=halves[:, :, :, 0, :],
                in1=halves[:, :, :, 1, :],
            )
            return rotated

        k_view = out_1.rearrange("(p j) h d -> p j (h d)", j=ROW_SETS)
        v_view = out_2.rearrange("(p j) h d -> p j (h d)", j=ROW_SETS)
        q_view = out_0.rearrange("(p j) h d -> p j (h d)", j=ROW_SETS)

        k_rows = keep.tile([P, ROW_SETS, N_KV], F32)
        planes_of = {}

        def turned_products(j, words, scales, first_col, on_gpsimd):
            acc = (aux_psum if on_gpsimd else rope_psum).tile([P, BANK], F32, tag="aux" if on_gpsimd else "acc", name="acc")
            for h in range(HEADS_PER_BANK):
                for g in range(PASSES):
                    nc.tensor.matmul_mx(
                        out=acc[:, P * h : P * (h + 1)],
                        lhsT=words[:, g, HEAD * h : HEAD * (h + 1)].bitcast(FP8X4),
                        lhsT_scale=scales[PLANE_STEP * g : P, first_col + HEAD * h : first_col + HEAD * (h + 1)],
                        rhs=x_codes[:, j, P * g : P * (g + 1)].bitcast(FP8X4),
                        rhs_scale=x_scales[:, j, P * g : P * (g + 1)],
                        start=(g == 0),
                        stop=(g == PASSES - 1),
                    )
            planes = turned_pool.tile([P, 2, BANK], F32, tag="planes")
            if on_gpsimd:
                sums = stage.tile([P, BANK], F32, tag="sums")
                nc.scalar.copy(out=sums[:], in_=acc[:])
                multiply(nc.gpsimd, planes[:], sums[:], turned_factors[:, j])
            else:
                multiply(nc.vector, planes[:], acc[:], turned_factors[:, j])
            return planes

        def turn_back(planes, out):
            back = aux_psum.tile([P, BANK], F32, tag="aux")
            for h in range(HEADS_PER_BANK):
                cols = slice(HEAD * h, HEAD * (h + 1))
                nc.tensor.matmul(
                    out=back[:, cols], lhsT=planes[:, 0, cols], rhs=ident[:], is_transpose=True, start=True, stop=False
                )
                nc.tensor.matmul(
                    out=back[:, cols], lhsT=planes[:, 1, cols], rhs=swap[:], is_transpose=True, start=False, stop=True
                )
            nc.scalar.copy(out=out, in_=back[:])

        def k_products(j, on_gpsimd=False):
            planes_of[j] = turned_products(j, wk, k_scales, 0, on_gpsimd)

        def k_finish(j):
            turn_back(planes_of[j], k_rows[:, j, :])

        def t_products(j, c, on_gpsimd=False):
            planes_of[j, c] = turned_products(j, wq[c], q_scales, BANK * c, on_gpsimd)

        def t_finish(j, c):
            rotated = back_pool.tile([P, BANK], F32, tag="back")
            turn_back(planes_of[j, c], rotated[:])
            nc.sync.dma_start(out=q_view[:, j, BANK * c : BANK * (c + 1)], in_=rotated[:])

        def k_store(first, count):
            rows = slice(first, first + count)
            nc.sync.dma_start(out=k_view[:, rows, :], in_=k_rows[:, rows, :])

        waiting = []

        def store_oldest():
            out_view, rotated = waiting.pop(0)
            nc.sync.dma_start(out=out_view, in_=rotated)

        gate_bytes = keep.tile([P, 64], U8, align_bytes=64)

        def gate_gpsimd(j):
            nc.gpsimd.tensor_copy(out=gate_bytes[:], in_=x_scales[:, j, 0:64])

        def q_products(banks):
            products = product_pool.tile([P, 2, BANK * len(banks)], F32, tag="products")
            for b, (j, c) in enumerate(banks):
                q_product(products, b, j, c)
            return products

        def q_product(products, b, j, c):
            acc = project(rope_psum, "acc", j, wq[c], q_scales, BANK * c)
            multiply(nc.vector, products[:, :, BANK * b : BANK * (b + 1)], acc[:], factors[:, j])

        def q_row_unit(j, first_bank, count):
            products = q_products([(j, c) for c in range(first_bank, first_bank + count)])
            width = BANK * count
            rotated = add_halves(nc.gpsimd, products, width)
            waiting.append((q_view[:, j, BANK * first_bank : BANK * first_bank + width], rotated[:]))

        def q_column_store(first, count, c, products):
            rotated = add_halves(nc.gpsimd, products, BANK * count)
            waiting.append((
                q_view[:, first : first + count, BANK * c : BANK * (c + 1)],
                rotated[:].rearrange("p (j n) -> p j n", n=BANK),
            ))

        def q_column_unit(first, count, c):
            q_column_store(first, count, c, q_products([(j, c) for j in range(first, first + count)]))

        v_rows = keep.tile([P, ROW_SETS, N_KV], F32)

        def v_pair(first):
            for j in (first, first + 1):
                acc = project(aux_psum, "aux", j, wv, v_scales, 0)
                nc.scalar.copy(out=v_rows[:, j, :], in_=acc[:])
            nc.sync.dma_start(out=v_view[:, first : first + 2, :], in_=v_rows[:, first : first + 2, :])

        keep_warm(4)
        early = [product_pool.tile([P, 2, 2 * BANK], F32, tag="products", name="early%d" % i) for i in range(2)]
        turn_halves(0)
        quantise_halves(0)
        turn_row_set(1)
        keep_warm(1)
        quantise(1)
        make_factors(*on_vector, 0, 4)
        q_product(early[0], 0, 0, 0)
        turn_row_set(2)
        turn_row_set(3)
        quantise(2)
        q_product(early[0], 1, 1, 0)
        quantise(3)
        turn_row_set(4)
        turn_row_set(5)
        quantise(4)
        q_product(early[1], 0, 2, 0)
        quantise(5)
        turn_row_set(6)
        turn_row_set(7)
        quantise(6)
        quantise(7)
        gate_gpsimd(7)
        q_product(early[1], 1, 3, 0)
        q_column_store(0, 2, 0, early[0])
        q_column_store(2, 2, 0, early[1])
        q_column_unit(0, 2, 1)
        make_crossed(*on_scalar, 0, half_sets)
        make_crossed(*on_scalar, half_sets, half_sets)
        q_column_unit(2, 2, 1)
        store_oldest()
        store_oldest()
        turn_factors(on_scalar[0], 0, half_sets)
        q_column_unit(0, 2, 2)
        store_oldest()
        v_pair(0)
        k_products(0)
        store_oldest()
        q_column_unit(2, 2, 2)
        store_oldest()
        make_factors(*on_scalar, half_sets, half_sets)
        q_column_unit(0, 2, 3)
        v_pair(2)
        k_products(1)
        k_finish(0)
        store_oldest()
        q_column_unit(2, 2, 3)
        store_oldest()
        turn_factors(on_scalar[0], half_sets, half_sets)
        q_row_unit(4, 0, 2)
        v_pair(4)
        k_products(2)
        k_finish(1)
        k_store(0, 2)
        store_oldest()
        q_row_unit(4, 2, 2)
        store_oldest()
        q_row_unit(5, 0, 2)
        v_pair(6)
        k_products(3)
        k_finish(2)
        store_oldest()
        q_row_unit(5, 2, 2)
        store_oldest()
        k_products(4)
        q_row_unit(6, 0, 2)
        k_finish(3)
        k_store(2, 2)
        store_oldest()
        k_products(5)
        q_row_unit(6, 2, 2)
        k_finish(4)
        store_oldest()
        k_products(6)
        q_row_unit(7, 0, 1)
        k_products(7)
        k_finish(5)
        k_store(4, 2)
        store_oldest()
        q_row_unit(7, 1, 1)
        before_last = q_products([(7, Q_BANKS - 2)])
        last_col = BANK * (Q_BANKS - 1)
        last_products = []
        acc = project(rope_psum, "acc", 7, wq[Q_BANKS - 1], q_scales, last_col)
        k_finish(6)
        k_store(6, 1)
        k_finish(7)
        k_store(7, 1)
        store_oldest()
        store_oldest()
        for part in range(2):
            part_cols = slice(BANK // 2 * part, BANK // 2 * (part + 1))
            products = product_pool.tile([P, 2, BANK // 2], F32, tag="products")
            multiply(nc.vector, products[:], acc[:, part_cols], factors[:, 7])
            last_products.append(products)
            if part == 0:
                rotated = add_halves(nc.vector, before_last, BANK)
                nc.sync.dma_start(out=q_view[:, 7, last_col - BANK : last_col], in_=rotated[:])
        for part in range(2):
            part_cols = slice(BANK // 2 * part, BANK // 2 * (part + 1))
            rotated = add_halves(nc.vector, last_products[part], BANK // 2)
            nc.sync.dma_start(
                out=q_view[:, 7, last_col + part_cols.start : last_col + part_cols.stop], in_=rotated[:]
            )
